import numpy as np
import ml_dtypes


def mxq(x, axis, fmt="e4m3"):
    dtype, down = {"e4m3": (ml_dtypes.float8_e4m3fn, 7), "e5m2": (ml_dtypes.float8_e5m2, 14)}[fmt]
    v = np.moveaxis(np.asarray(x, np.float32).astype(ml_dtypes.bfloat16).astype(np.float64), axis, -1)
    blocks = v.reshape(v.shape[:-1] + (-1, 32))
    amax = np.abs(blocks).max(-1, keepdims=True)
    byte = np.maximum(np.where(amax > 0, np.frexp(amax)[1] - 1 + 127, 0) - down, 1)
    scale = np.exp2(byte - 127.0)
    codes = (blocks / scale).astype(np.float32).astype(dtype).astype(np.float64)
    return np.moveaxis((codes * scale).reshape(v.shape), -1, axis)


WIDE = False


def mx_kscale(k):
    if not WIDE:
        return np.ones(k)
    levels = np.array([10, -10, 5, -5, 0])
    a = np.random.permutation(np.resize(levels, k // 512 * 4)).reshape(k // 512, 4)
    idx = np.arange(k)
    return np.exp2(a[idx // 512, idx % 128 // 32])


BF16 = ml_dtypes.bfloat16


def bf(x):
    return np.asarray(x, np.float32).astype(BF16)


def f64(x):
    return np.asarray(x).astype(np.float64)


M, J, L, H, K, I, S = 8, 1024, 28, 28, 3, 256, 2
SHIFT = 1


def setup_inputs():
    s = mx_kscale(J)
    x = np.random.standard_normal((M, J, L, H)) * s[None, :, None, None]
    return {"x": bf(x.reshape(M, J * L, H)),
            "w1": bf(np.random.standard_normal((I, S))),
            "w2": bf(np.random.standard_normal((J, K, I)) / np.sqrt(J * K) / s[:, None, None])}


def reference(x, w1, w2):
    xq = mxq(f64(x).reshape(M, J, L, H).transpose(0, 2, 3, 1).reshape(M * L * H, J), 1, "e4m3")
    y = [(xq @ mxq(f64(w2)[:, k, :], 0, "e4m3")).reshape(M, L, H, I) for k in range(K)]
    t4 = sum(np.pad(y[k], ((0, 0), (0, 0), (1, 1), (0, 0)))[:, :, k:k + H, :] for k in range(K))
    t5 = t4[..., None] * f64(w1)
    t6 = np.roll(t5, SHIFT, axis=1)
    t6 = np.transpose(t6, (0, 2, 3, 1, 4)).reshape(M, H, I, L * S)
    t6 = np.roll(t6, SHIFT, axis=3)
    t6 = t6.reshape(M, H, I, L, S).sum(axis=4)
    return np.transpose(t6, (0, 2, 3, 1))

@@ -1,0 +1,198 @@
+from contextlib import ExitStack
+
+import concourse.mybir as mybir
+
+FP8X4 = mybir.dt.float8_e4m3fn_x4
+BF16 = mybir.dt.bfloat16
+F32 = mybir.dt.float32
+U32 = mybir.dt.uint32
+U8 = mybir.dt.uint8
+I32 = mybir.dt.int32
+ALU = mybir.AluOpType
+ACT = mybir.ActivationFunctionType
+
+M, J, L, H, K, I = 8, 1024, 28, 28, 3, 256
+FLOPS = 2 * M * L * H * J * K * I
+BYTES = 2 * M * J * L * H + 2 * J * K * I + 2 * I * 2 + 4 * M * I * L * H
+
+P = 128
+GROUPS = 4
+ROW = 64
+NROWS = 30
+BANKS = ((0, 8), (8, 8), (16, 8), (24, 4))
+
+
+def tile_kernel_generated_1_t_kernel(tc, x, w1, w2, out):
+    nc = tc.nc
+    with ExitStack() as ctx:
+        const = ctx.enter_context(tc.tile_pool(name="const", bufs=1))
+        rawp = ctx.enter_context(tc.tile_pool(name="rawp", bufs=8))
+        outp = ctx.enter_context(tc.tile_pool(name="outp", bufs=4))
+        psum = ctx.enter_context(tc.psum_pool(name="psum", bufs=8))
+
+        w1b = const.tile([P, 2, 2], BF16, name="w1b")
+        w1f = const.tile([P, 2, 2], F32, name="w1f")
+        w2raw = [const.tile([P, 3072], BF16, name="w2raw%d" % c) for c in range(2)]
+        w2g = [const.tile([P, 3072], BF16, name="w2g%d" % c, align_bytes=64) for c in range(2)]
+        wq = const.tile([P, 2, 768], U32, name="wq", align_bytes=64)
+        ws = const.tile([P, 2, 768], U8, name="ws", align_bytes=64)
+        gt = {}
+        xq = {}
+        xs = {}
+        for s in range(2):
+            for c in range(2):
+                gt[(s, c)] = const.tile([P, 28 * ROW * 4], BF16, name="gt%d%d" % (s, c), align_bytes=64)
+                xq[(s, c)] = const.tile([P, NROWS * ROW], U32, name="xq%d%d" % (s, c), align_bytes=64)
+                xs[(s, c)] = const.tile([P, NROWS * ROW], U8, name="xs%d%d" % (s, c), align_bytes=64)
+        ab = [const.tile([P, ROW, 28], F32, name="ab%d" % h) for h in range(2)]
+
+        raws = {}
+
+        def load_w2(c):
+            nc.sync.dma_start(
+                out=w2raw[c][:],
+                in_=w2[c * 512:(c + 1) * 512].rearrange("(p t) k i -> p (t k i)", p=P),
+            )
+
+        def load_x(g, c, mm):
+            raw = rawp.tile([P, 3136], BF16, name="raw", tag="raw")
+            nc.sync.dma_start(
+                out=raw[:],
+                in_=x[2 * g + mm, c * 14336:(c + 1) * 14336, :].rearrange("(p r) n -> p (r n)", p=P),
+            )
+            raws[(g, c, mm)] = raw
+
+        def load_group(g):
+            for c in range(2):
+                for mm in range(2):
+                    load_x(g, c, mm)
+
+        nc.scalar.dma_start(out=w1b[:], in_=w1.rearrange("(h p) s -> p h s", p=P))
+        load_w2(0)
+        load_x(0, 0, 0)
+        load_x(0, 0, 1)
+        load_w2(1)
+        load_x(0, 1, 0)
+        load_x(0, 1, 1)
+        load_group(1)
+
+        for key in sorted(gt):
+            nc.vector.memset(gt[key][:].rearrange("p (r s) -> p r s", s=128)[:, :, 112:128], 0.0)
+            for r in (0, NROWS - 1):
+                nc.vector.memset(xq[key][:, r * ROW:(r + 1) * ROW].bitcast(I32), 0)
+                nc.vector.memset(xs[key][:, r * ROW:(r + 1) * ROW].bitcast(I32), 0)
+        for h in range(2):
+            nc.vector.memset(ab[h][:, 0, :], 0.0)
+        nc.vector.tensor_copy(out=w1f[:], in_=w1b[:])
+
+        def prep_w2(c):
+            src = w2raw[c][:].rearrange("p (t q i) -> p q t i", t=4, i=4)
+            dst = w2g[c][:].rearrange("p (q i t) -> p q t i", i=4, t=4)
+            nc.vector.tensor_copy(out=dst[:, 0:128], in_=src[:, 0:128])
+            nc.scalar.copy(out=dst[:, 128:192], in_=src[:, 128:192])
+            nc.vector.quantize_mx(out=wq[:, c, 0:512].bitcast(FP8X4), scales=ws[:, c, 0:512], in_=w2g[c][:, 0:2048])
+            nc.vector.quantize_mx(out=wq[:, c, 512:768].bitcast(FP8X4), scales=ws[:, c, 512:768], in_=w2g[c][:, 2048:3072])
+
+        def regroup(copy, g, c, mm, b0, b1):
+            src = raws[(g, c, mm)][:].rearrange("p (t l b i) -> p b l t i", t=4, l=28, b=7, i=4)
+            dst = gt[(g % 2, c)][:].rearrange("p (b i m s t) -> p m b s t i", b=7, i=4, m=2, s=32, t=4)
+            copy(out=dst[:, mm, b0:b1, 0:28, :, :], in_=src[:, b0:b1])
+
+        def quant(g, c, r0, nr):
+            key = (g % 2, c)
+            a = (1 + r0) * ROW
+            b = (1 + r0 + nr) * ROW
+            nc.vector.quantize_mx(
+                out=xq[key][:, a:b].bitcast(FP8X4),
+                scales=xs[key][:, a:b],
+                in_=gt[key][:, r0 * ROW * 4:(r0 + nr) * ROW * 4],
+            )
+
+        def quant_all(g, c):
+            for r0, nr in BANKS:
+                quant(g, c, r0, nr)
+
+        banks = {}
+
+        def passes(g, j, c):
+            h, nb = j // 4, j % 4
+            n0, nr = BANKS[nb]
+            if c == 0:
+                banks[(g, j)] = psum.tile([P, 512], F32, name="ps", tag="ps")
+            ps = banks[(g, j)]
+            key = (g % 2, c)
+            width = nr * ROW
+            for k in range(K):
+                col = k * 256 + h * 128
+                a = (n0 + k) * ROW
+                nc.tensor.matmul_mx(
+                    out=ps[:, 0:width],
+                    lhsT=wq[:, c, col:col + 128].bitcast(FP8X4),
+                    lhsT_scale=ws[:, c, col:col + 128],
+                    rhs=xq[key][:, a:a + width].bitcast(FP8X4),
+                    rhs_scale=xs[key][:, a:a + width],
+                    start=(c == 0 and k == 0),
+                    stop=(c == 1 and k == K - 1),
+                )
+
+        outs = {}
+
+        def epilogue(g, j):
+            h, nb = j // 4, j % 4
+            n0, nr = BANKS[nb]
+            if nb == 0:
+                outs[(g, h)] = outp.tile([P, ROW, 28], F32, name="ot", tag="ot")
+            ot = outs[(g, h)]
+            t4 = banks[(g, j)][:, 0:nr * ROW].rearrange("p (n f) -> p f n", f=ROW)[:, 0:60, :]
+            nc.scalar.activation(out=ab[h][:, 1:61, n0:n0 + nr], in_=t4, func=ACT.Copy, scale=w1f[:, h, 1:2])
+            nc.vector.scalar_tensor_tensor(
+                out=ot[:, 1:61, n0:n0 + nr], in0=t4, scalar=w1f[:, h, 0:1],
+                in1=ab[h][:, 0:60, n0:n0 + nr], op0=ALU.mult, op1=ALU.add,
+            )
+
+        def finish(g, h):
+            ov = outs[(g, h)][:].rearrange("p (m s) n -> p m s n", s=32)
+            av = ab[h][:].rearrange("p (m s) n -> p m s n", s=32)
+            nc.vector.tensor_tensor(out=ov[:, :, 1, :], in0=ov[:, :, 1, :], in1=av[:, :, 28, :], op=ALU.add)
+            nc.vector.tensor_copy(out=ov[:, :, 0, :], in_=ov[:, :, 28, :])
+            nc.sync.dma_start(
+                out=out[2 * g:2 * g + 2, h * P:(h + 1) * P].rearrange("m p l n -> p m (l n)"),
+                in_=ov[:, :, 0:28, :].rearrange("p m s n -> p m (s n)"),
+            )
+
+        vcopy = nc.vector.tensor_copy
+        scopy = nc.scalar.copy
+
+        for c in range(2):
+            prep_w2(c)
+            for mm in range(2):
+                regroup(vcopy, 0, c, mm, 0, 4)
+                regroup(scopy, 0, c, mm, 4, 7)
+            quant_all(0, c)
+        load_group(2)
+
+        for g in range(GROUPS):
+            nxt = g + 1 < GROUPS
+            if nxt:
+                regroup(vcopy, g + 1, 0, 0, 0, 7)
+                regroup(scopy, g + 1, 1, 0, 0, 4)
+                regroup(vcopy, g + 1, 0, 1, 0, 7)
+                regroup(scopy, g + 1, 1, 0, 4, 7)
+            for j in range(8):
+                passes(g, j, 0)
+            if nxt:
+                quant_all(g + 1, 0)
+            for j in range(8):
+                passes(g, j, 1)
+                epilogue(g, j)
+                if nxt and j == 1:
+                    regroup(scopy, g + 1, 1, 1, 0, 4)
+                if nxt and j == 4:
+                    regroup(scopy, g + 1, 1, 1, 4, 7)
+                    if g + 3 < GROUPS:
+                        load_group(g + 3)
+                if j == 3:
+                    finish(g, 0)
+                if nxt and j == 6:
+                    quant_all(g + 1, 1)
+            finish(g, 1)

@@ -19,7 +19,9 @@ P = 128
 GROUPS = 4
 ROW = 64
 NROWS = 30
-BANKS = ((0, 8), (8, 8), (16, 8), (24, 4))
+QBLOCKS = ((0, 8), (8, 8), (16, 8), (24, 4))
+BANKS_FIRST = ((0, 4), (4, 8), (12, 8), (20, 8))
+BANKS_REST = ((0, 8), (8, 8), (16, 8), (24, 4))
 
 
 def tile_kernel_generated_1_t_kernel(tc, x, w1, w2, out):
@@ -109,14 +111,20 @@ def tile_kernel_generated_1_t_kernel(tc, x, w1, w2, out):
             )
 
         def quant_all(g, c):
-            for r0, nr in BANKS:
+            for r0, nr in QBLOCKS:
                 quant(g, c, r0, nr)
 
         banks = {}
 
-        def passes(g, j, c):
+        def where(g, j):
+            if g == 0:
+                h, nb = j % 2, j // 2
+                return h, nb, BANKS_FIRST[nb]
             h, nb = j // 4, j % 4
-            n0, nr = BANKS[nb]
+            return h, nb, BANKS_REST[nb]
+
+        def passes(g, j, c):
+            h, nb, (n0, nr) = where(g, j)
             if c == 0:
                 banks[(g, j)] = psum.tile([P, 512], F32, name="ps", tag="ps")
             ps = banks[(g, j)]
@@ -138,8 +146,7 @@ def tile_kernel_generated_1_t_kernel(tc, x, w1, w2, out):
         outs = {}
 
         def epilogue(g, j):
-            h, nb = j // 4, j % 4
-            n0, nr = BANKS[nb]
+            h, nb, (n0, nr) = where(g, j)
             if nb == 0:
                 outs[(g, h)] = outp.tile([P, ROW, 28], F32, name="ot", tag="ot")
             ot = outs[(g, h)]
@@ -153,8 +160,9 @@ def tile_kernel_generated_1_t_kernel(tc, x, w1, w2, out):
         def finish(g, h):
             ov = outs[(g, h)][:].rearrange("p (m s) n -> p m s n", s=32)
             av = ab[h][:].rearrange("p (m s) n -> p m s n", s=32)
-            nc.vector.tensor_tensor(out=ov[:, :, 1, :], in0=ov[:, :, 1, :], in1=av[:, :, 28, :], op=ALU.add)
-            nc.vector.tensor_copy(out=ov[:, :, 0, :], in_=ov[:, :, 28, :])
+            eng = nc.vector if (g == GROUPS - 1 and h == 1) else nc.gpsimd
+            eng.tensor_tensor(out=ov[:, :, 1, :], in0=ov[:, :, 1, :], in1=av[:, :, 28, :], op=ALU.add)
+            eng.tensor_copy(out=ov[:, :, 0, :], in_=ov[:, :, 28, :])
             nc.sync.dma_start(
                 out=out[2 * g:2 * g + 2, h * P:(h + 1) * P].rearrange("m p l n -> p m (l n)"),
                 in_=ov[:, :, 0:28, :].rearrange("p m s n -> p m (s n)"),
@@ -163,21 +171,43 @@ def tile_kernel_generated_1_t_kernel(tc, x, w1, w2, out):
         vcopy = nc.vector.tensor_copy
         scopy = nc.scalar.copy
 
-        for c in range(2):
-            prep_w2(c)
-            for mm in range(2):
-                regroup(vcopy, 0, c, mm, 0, 4)
-                regroup(scopy, 0, c, mm, 4, 7)
-            quant_all(0, c)
+        def regroup_pool(g, c, mm, b0, b1):
+            src = raws[(g, c, mm)][:].rearrange("p (t l b i) -> p b l t i", t=4, l=28, b=7, i=4)
+            dst = gt[(g % 2, c)][:].rearrange("p (b i m s t) -> p m b s t i", b=7, i=4, m=2, s=32, t=4)
+            for b in range(b0, b1):
+                nc.gpsimd.tensor_scalar(
+                    out=dst[:, mm, b, 0:28, :, :], in0=src[:, b], scalar1=1.0, scalar2=0.0,
+                    op0=ALU.mult, op1=ALU.add,
+                )
+
+        prep_w2(0)
+        regroup(vcopy, 0, 0, 0, 0, 2)
+        regroup(scopy, 0, 0, 0, 2, 4)
+        regroup(vcopy, 0, 0, 0, 4, 6)
+        regroup(scopy, 0, 0, 0, 6, 7)
+        regroup(vcopy, 0, 0, 1, 0, 2)
+        regroup(scopy, 0, 0, 1, 2, 4)
+        quant(0, 0, 0, 8)
+        regroup(vcopy, 0, 0, 1, 4, 6)
+        regroup(scopy, 0, 0, 1, 6, 7)
+        quant(0, 0, 8, 8)
+        quant(0, 0, 16, 8)
+        quant(0, 0, 24, 4)
+        prep_w2(1)
+        for mm in range(2):
+            regroup(vcopy, 0, 1, mm, 0, 4)
+            regroup(scopy, 0, 1, mm, 4, 7)
+        quant_all(0, 1)
         load_group(2)
 
         for g in range(GROUPS):
             nxt = g + 1 < GROUPS
             if nxt:
                 regroup(vcopy, g + 1, 0, 0, 0, 7)
+                regroup(scopy, g + 1, 0, 1, 5, 7)
+                regroup(vcopy, g + 1, 0, 1, 0, 5)
                 regroup(scopy, g + 1, 1, 0, 0, 4)
-                regroup(vcopy, g + 1, 0, 1, 0, 7)
-                regroup(scopy, g + 1, 1, 0, 4, 7)
+                regroup_pool(g + 1, 1, 1, 3, 7)
             for j in range(8):
                 passes(g, j, 0)
             if nxt:
@@ -186,13 +216,15 @@ def tile_kernel_generated_1_t_kernel(tc, x, w1, w2, out):
                 passes(g, j, 1)
                 epilogue(g, j)
                 if nxt and j == 1:
-                    regroup(scopy, g + 1, 1, 1, 0, 4)
+                    regroup(scopy, g + 1, 1, 0, 4, 7)
                 if nxt and j == 4:
-                    regroup(scopy, g + 1, 1, 1, 4, 7)
+                    regroup(scopy, g + 1, 1, 1, 0, 3)
                     if g + 3 < GROUPS:
                         load_group(g + 3)
-                if j == 3:
+                if j == 3 and g > 0:
                     finish(g, 0)
                 if nxt and j == 6:
                     quant_all(g + 1, 1)
+            if g == 0:
+                finish(g, 0)
             finish(g, 1)

@@ -90,8 +90,8 @@ def tile_kernel_generated_1_t_kernel(tc, x, w1, w2, out):
         def prep_w2(c):
             src = w2raw[c][:].rearrange("p (t q i) -> p q t i", t=4, i=4)
             dst = w2g[c][:].rearrange("p (q i t) -> p q t i", i=4, t=4)
-            nc.vector.tensor_copy(out=dst[:, 0:128], in_=src[:, 0:128])
-            nc.scalar.copy(out=dst[:, 128:192], in_=src[:, 128:192])
+            nc.vector.tensor_copy(out=dst[:, 0:96], in_=src[:, 0:96])
+            nc.scalar.copy(out=dst[:, 96:192], in_=src[:, 96:192])
             nc.vector.quantize_mx(out=wq[:, c, 0:512].bitcast(FP8X4), scales=ws[:, c, 0:512], in_=w2g[c][:, 0:2048])
             nc.vector.quantize_mx(out=wq[:, c, 512:768].bitcast(FP8X4), scales=ws[:, c, 512:768], in_=w2g[c][:, 2048:3072])
 
@@ -171,15 +171,6 @@ def tile_kernel_generated_1_t_kernel(tc, x, w1, w2, out):
         vcopy = nc.vector.tensor_copy
         scopy = nc.scalar.copy
 
-        def regroup_pool(g, c, mm, b0, b1):
-            src = raws[(g, c, mm)][:].rearrange("p (t l b i) -> p b l t i", t=4, l=28, b=7, i=4)
-            dst = gt[(g % 2, c)][:].rearrange("p (b i m s t) -> p m b s t i", b=7, i=4, m=2, s=32, t=4)
-            for b in range(b0, b1):
-                nc.gpsimd.tensor_scalar(
-                    out=dst[:, mm, b, 0:28, :, :], in0=src[:, b], scalar1=1.0, scalar2=0.0,
-                    op0=ALU.mult, op1=ALU.add,
-                )
-
         prep_w2(0)
         regroup(vcopy, 0, 0, 0, 0, 2)
         regroup(scopy, 0, 0, 0, 2, 4)
@@ -195,8 +186,8 @@ def tile_kernel_generated_1_t_kernel(tc, x, w1, w2, out):
         quant(0, 0, 24, 4)
         prep_w2(1)
         for mm in range(2):
-            regroup(vcopy, 0, 1, mm, 0, 4)
-            regroup(scopy, 0, 1, mm, 4, 7)
+            regroup(vcopy, 0, 1, mm, 0, 3)
+            regroup(scopy, 0, 1, mm, 3, 7)
         quant_all(0, 1)
         load_group(2)
 
@@ -204,10 +195,9 @@ def tile_kernel_generated_1_t_kernel(tc, x, w1, w2, out):
             nxt = g + 1 < GROUPS
             if nxt:
                 regroup(vcopy, g + 1, 0, 0, 0, 7)
-                regroup(scopy, g + 1, 0, 1, 5, 7)
-                regroup(vcopy, g + 1, 0, 1, 0, 5)
                 regroup(scopy, g + 1, 1, 0, 0, 4)
-                regroup_pool(g + 1, 1, 1, 3, 7)
+                regroup(vcopy, g + 1, 0, 1, 0, 7)
+                regroup(scopy, g + 1, 1, 0, 4, 7)
             for j in range(8):
                 passes(g, j, 0)
             if nxt:
@@ -216,9 +206,9 @@ def tile_kernel_generated_1_t_kernel(tc, x, w1, w2, out):
                 passes(g, j, 1)
                 epilogue(g, j)
                 if nxt and j == 1:
-                    regroup(scopy, g + 1, 1, 0, 4, 7)
+                    regroup(scopy, g + 1, 1, 1, 0, 4)
                 if nxt and j == 4:
-                    regroup(scopy, g + 1, 1, 1, 0, 3)
+                    regroup(scopy, g + 1, 1, 1, 4, 7)
                     if g + 3 < GROUPS:
                         load_group(g + 3)
                 if j == 3 and g > 0:

@@ -19,9 +19,7 @@ P = 128
 GROUPS = 4
 ROW = 64
 NROWS = 30
-QBLOCKS = ((0, 8), (8, 8), (16, 8), (24, 4))
-BANKS_FIRST = ((0, 4), (4, 8), (12, 8), (20, 8))
-BANKS_REST = ((0, 8), (8, 8), (16, 8), (24, 4))
+BANKS = ((0, 8), (8, 8), (16, 8), (24, 4))
 
 
 def tile_kernel_generated_1_t_kernel(tc, x, w1, w2, out):
@@ -90,8 +88,8 @@ def tile_kernel_generated_1_t_kernel(tc, x, w1, w2, out):
         def prep_w2(c):
             src = w2raw[c][:].rearrange("p (t q i) -> p q t i", t=4, i=4)
             dst = w2g[c][:].rearrange("p (q i t) -> p q t i", i=4, t=4)
-            nc.vector.tensor_copy(out=dst[:, 0:96], in_=src[:, 0:96])
-            nc.scalar.copy(out=dst[:, 96:192], in_=src[:, 96:192])
+            nc.vector.tensor_copy(out=dst[:, 0:128], in_=src[:, 0:128])
+            nc.scalar.copy(out=dst[:, 128:192], in_=src[:, 128:192])
             nc.vector.quantize_mx(out=wq[:, c, 0:512].bitcast(FP8X4), scales=ws[:, c, 0:512], in_=w2g[c][:, 0:2048])
             nc.vector.quantize_mx(out=wq[:, c, 512:768].bitcast(FP8X4), scales=ws[:, c, 512:768], in_=w2g[c][:, 2048:3072])
 
@@ -111,20 +109,14 @@ def tile_kernel_generated_1_t_kernel(tc, x, w1, w2, out):
             )
 
         def quant_all(g, c):
-            for r0, nr in QBLOCKS:
+            for r0, nr in BANKS:
                 quant(g, c, r0, nr)
 
         banks = {}
 
-        def where(g, j):
-            if g == 0:
-                h, nb = j % 2, j // 2
-                return h, nb, BANKS_FIRST[nb]
-            h, nb = j // 4, j % 4
-            return h, nb, BANKS_REST[nb]
-
         def passes(g, j, c):
-            h, nb, (n0, nr) = where(g, j)
+            h, nb = j // 4, j % 4
+            n0, nr = BANKS[nb]
             if c == 0:
                 banks[(g, j)] = psum.tile([P, 512], F32, name="ps", tag="ps")
             ps = banks[(g, j)]
@@ -146,7 +138,8 @@ def tile_kernel_generated_1_t_kernel(tc, x, w1, w2, out):
         outs = {}
 
         def epilogue(g, j):
-            h, nb, (n0, nr) = where(g, j)
+            h, nb = j // 4, j % 4
+            n0, nr = BANKS[nb]
             if nb == 0:
                 outs[(g, h)] = outp.tile([P, ROW, 28], F32, name="ot", tag="ot")
             ot = outs[(g, h)]
@@ -160,9 +153,8 @@ def tile_kernel_generated_1_t_kernel(tc, x, w1, w2, out):
         def finish(g, h):
             ov = outs[(g, h)][:].rearrange("p (m s) n -> p m s n", s=32)
             av = ab[h][:].rearrange("p (m s) n -> p m s n", s=32)
-            eng = nc.vector if (g == GROUPS - 1 and h == 1) else nc.gpsimd
-            eng.tensor_tensor(out=ov[:, :, 1, :], in0=ov[:, :, 1, :], in1=av[:, :, 28, :], op=ALU.add)
-            eng.tensor_copy(out=ov[:, :, 0, :], in_=ov[:, :, 28, :])
+            nc.vector.tensor_tensor(out=ov[:, :, 1, :], in0=ov[:, :, 1, :], in1=av[:, :, 28, :], op=ALU.add)
+            nc.vector.tensor_copy(out=ov[:, :, 0, :], in_=ov[:, :, 28, :])
             nc.sync.dma_start(
                 out=out[2 * g:2 * g + 2, h * P:(h + 1) * P].rearrange("m p l n -> p m (l n)"),
                 in_=ov[:, :, 0:28, :].rearrange("p m s n -> p m (s n)"),
@@ -171,24 +163,12 @@ def tile_kernel_generated_1_t_kernel(tc, x, w1, w2, out):
         vcopy = nc.vector.tensor_copy
         scopy = nc.scalar.copy
 
-        prep_w2(0)
-        regroup(vcopy, 0, 0, 0, 0, 2)
-        regroup(scopy, 0, 0, 0, 2, 4)
-        regroup(vcopy, 0, 0, 0, 4, 6)
-        regroup(scopy, 0, 0, 0, 6, 7)
-        regroup(vcopy, 0, 0, 1, 0, 2)
-        regroup(scopy, 0, 0, 1, 2, 4)
-        quant(0, 0, 0, 8)
-        regroup(vcopy, 0, 0, 1, 4, 6)
-        regroup(scopy, 0, 0, 1, 6, 7)
-        quant(0, 0, 8, 8)
-        quant(0, 0, 16, 8)
-        quant(0, 0, 24, 4)
-        prep_w2(1)
-        for mm in range(2):
-            regroup(vcopy, 0, 1, mm, 0, 3)
-            regroup(scopy, 0, 1, mm, 3, 7)
-        quant_all(0, 1)
+        for c in range(2):
+            prep_w2(c)
+            for mm in range(2):
+                regroup(vcopy, 0, c, mm, 0, 4)
+                regroup(scopy, 0, c, mm, 4, 7)
+            quant_all(0, c)
         load_group(2)
 
         for g in range(GROUPS):
@@ -198,6 +178,7 @@ def tile_kernel_generated_1_t_kernel(tc, x, w1, w2, out):
                 regroup(scopy, g + 1, 1, 0, 0, 4)
                 regroup(vcopy, g + 1, 0, 1, 0, 7)
                 regroup(scopy, g + 1, 1, 0, 4, 7)
+                regroup(vcopy, g + 1, 1, 1, 5, 7)
             for j in range(8):
                 passes(g, j, 0)
             if nxt:
@@ -206,15 +187,13 @@ def tile_kernel_generated_1_t_kernel(tc, x, w1, w2, out):
                 passes(g, j, 1)
                 epilogue(g, j)
                 if nxt and j == 1:
-                    regroup(scopy, g + 1, 1, 1, 0, 4)
+                    regroup(scopy, g + 1, 1, 1, 0, 3)
                 if nxt and j == 4:
-                    regroup(scopy, g + 1, 1, 1, 4, 7)
+                    regroup(scopy, g + 1, 1, 1, 3, 5)
                     if g + 3 < GROUPS:
                         load_group(g + 3)
-                if j == 3 and g > 0:
+                if j == 3:
                     finish(g, 0)
                 if nxt and j == 6:
                     quant_all(g + 1, 1)
-            if g == 0:
-                finish(g, 0)
             finish(g, 1)

@@ -88,8 +88,8 @@ def tile_kernel_generated_1_t_kernel(tc, x, w1, w2, out):
         def prep_w2(c):
             src = w2raw[c][:].rearrange("p (t q i) -> p q t i", t=4, i=4)
             dst = w2g[c][:].rearrange("p (q i t) -> p q t i", i=4, t=4)
-            nc.vector.tensor_copy(out=dst[:, 0:128], in_=src[:, 0:128])
-            nc.scalar.copy(out=dst[:, 128:192], in_=src[:, 128:192])
+            nc.vector.tensor_copy(out=dst[:, 0:96], in_=src[:, 0:96])
+            nc.scalar.copy(out=dst[:, 96:192], in_=src[:, 96:192])
             nc.vector.quantize_mx(out=wq[:, c, 0:512].bitcast(FP8X4), scales=ws[:, c, 0:512], in_=w2g[c][:, 0:2048])
             nc.vector.quantize_mx(out=wq[:, c, 512:768].bitcast(FP8X4), scales=ws[:, c, 512:768], in_=w2g[c][:, 2048:3072])
 
@@ -166,8 +166,8 @@ def tile_kernel_generated_1_t_kernel(tc, x, w1, w2, out):
         for c in range(2):
             prep_w2(c)
             for mm in range(2):
-                regroup(vcopy, 0, c, mm, 0, 4)
-                regroup(scopy, 0, c, mm, 4, 7)
+                regroup(vcopy, 0, c, mm, 0, 4 - c)
+                regroup(scopy, 0, c, mm, 4 - c, 7)
             quant_all(0, c)
         load_group(2)
 
@@ -176,9 +176,9 @@ def tile_kernel_generated_1_t_kernel(tc, x, w1, w2, out):
             if nxt:
                 regroup(vcopy, g + 1, 0, 0, 0, 7)
                 regroup(scopy, g + 1, 1, 0, 0, 4)
-                regroup(vcopy, g + 1, 0, 1, 0, 7)
+                regroup(vcopy, g + 1, 0, 1, 0, 6)
+                regroup(scopy, g + 1, 0, 1, 6, 7)
                 regroup(scopy, g + 1, 1, 0, 4, 7)
-                regroup(vcopy, g + 1, 1, 1, 5, 7)
             for j in range(8):
                 passes(g, j, 0)
             if nxt:
@@ -187,9 +187,9 @@ def tile_kernel_generated_1_t_kernel(tc, x, w1, w2, out):
                 passes(g, j, 1)
                 epilogue(g, j)
                 if nxt and j == 1:
-                    regroup(scopy, g + 1, 1, 1, 0, 3)
+                    regroup(scopy, g + 1, 1, 1, 0, 4)
                 if nxt and j == 4:
-                    regroup(scopy, g + 1, 1, 1, 3, 5)
+                    regroup(scopy, g + 1, 1, 1, 4, 7)
                     if g + 3 < GROUPS:
                         load_group(g + 3)
                 if j == 3:

@@ -34,16 +34,16 @@ def tile_kernel_generated_1_t_kernel(tc, x, w1, w2, out):
         w1f = const.tile([P, 2, 2], F32, name="w1f")
         w2raw = [const.tile([P, 3072], BF16, name="w2raw%d" % c) for c in range(2)]
         w2g = [const.tile([P, 3072], BF16, name="w2g%d" % c, align_bytes=64) for c in range(2)]
-        wq = const.tile([P, 2, 768], U32, name="wq", align_bytes=64)
-        ws = const.tile([P, 2, 768], U8, name="ws", align_bytes=64)
+        wq = const.tile([P, 48 + 2 * 768], U32, name="wq", align_bytes=256)
+        ws = const.tile([P, 12 * 256], U8, name="ws", align_bytes=256)
         gt = {}
         xq = {}
         xs = {}
         for s in range(2):
             for c in range(2):
                 gt[(s, c)] = const.tile([P, 28 * ROW * 4], BF16, name="gt%d%d" % (s, c), align_bytes=64)
-                xq[(s, c)] = const.tile([P, NROWS * ROW], U32, name="xq%d%d" % (s, c), align_bytes=64)
-                xs[(s, c)] = const.tile([P, NROWS * ROW], U8, name="xs%d%d" % (s, c), align_bytes=64)
+                xq[(s, c)] = const.tile([P, NROWS * ROW], U32, name="xq%d%d" % (s, c), align_bytes=256)
+                xs[(s, c)] = const.tile([P, NROWS * ROW], U8, name="xs%d%d" % (s, c), align_bytes=256)
         ab = [const.tile([P, ROW, 28], F32, name="ab%d" % h) for h in range(2)]
 
         raws = {}
@@ -90,8 +90,13 @@ def tile_kernel_generated_1_t_kernel(tc, x, w1, w2, out):
             dst = w2g[c][:].rearrange("p (q i t) -> p q t i", i=4, t=4)
             nc.vector.tensor_copy(out=dst[:, 0:96], in_=src[:, 0:96])
             nc.scalar.copy(out=dst[:, 96:192], in_=src[:, 96:192])
-            nc.vector.quantize_mx(out=wq[:, c, 0:512].bitcast(FP8X4), scales=ws[:, c, 0:512], in_=w2g[c][:, 0:2048])
-            nc.vector.quantize_mx(out=wq[:, c, 512:768].bitcast(FP8X4), scales=ws[:, c, 512:768], in_=w2g[c][:, 2048:3072])
+            for u in range(6):
+                wa = 48 + c * 768 + u * 128
+                sa = (c * 6 + u) * 256
+                nc.vector.quantize_mx(
+                    out=wq[:, wa:wa + 128].bitcast(FP8X4), scales=ws[:, sa:sa + 128],
+                    in_=w2g[c][:, u * 512:(u + 1) * 512],
+                )
 
         def regroup(copy, g, c, mm, b0, b1):
             src = raws[(g, c, mm)][:].rearrange("p (t l b i) -> p b l t i", t=4, l=28, b=7, i=4)
@@ -127,8 +132,8 @@ def tile_kernel_generated_1_t_kernel(tc, x, w1, w2, out):
                 a = (n0 + k) * ROW
                 nc.tensor.matmul_mx(
                     out=ps[:, 0:width],
-                    lhsT=wq[:, c, col:col + 128].bitcast(FP8X4),
-                    lhsT_scale=ws[:, c, col:col + 128],
+                    lhsT=wq[:, 48 + c * 768 + col:48 + c * 768 + col + 128].bitcast(FP8X4),
+                    lhsT_scale=ws[:, (c * 6 + col // 128) * 256:(c * 6 + col // 128) * 256 + 128],
                     rhs=xq[key][:, a:a + width].bitcast(FP8X4),
                     rhs_scale=xs[key][:, a:a + width],
                     start=(c == 0 and k == 0),

@@ -34,16 +34,16 @@ def tile_kernel_generated_1_t_kernel(tc, x, w1, w2, out):
         w1f = const.tile([P, 2, 2], F32, name="w1f")
         w2raw = [const.tile([P, 3072], BF16, name="w2raw%d" % c) for c in range(2)]
         w2g = [const.tile([P, 3072], BF16, name="w2g%d" % c, align_bytes=64) for c in range(2)]
-        wq = const.tile([P, 48 + 2 * 768], U32, name="wq", align_bytes=256)
-        ws = const.tile([P, 12 * 256], U8, name="ws", align_bytes=256)
+        wq = const.tile([P, 2, 768], U32, name="wq", align_bytes=64)
+        ws = const.tile([P, 2, 768], U8, name="ws", align_bytes=64)
         gt = {}
         xq = {}
         xs = {}
         for s in range(2):
             for c in range(2):
                 gt[(s, c)] = const.tile([P, 28 * ROW * 4], BF16, name="gt%d%d" % (s, c), align_bytes=64)
-                xq[(s, c)] = const.tile([P, NROWS * ROW], U32, name="xq%d%d" % (s, c), align_bytes=256)
-                xs[(s, c)] = const.tile([P, NROWS * ROW], U8, name="xs%d%d" % (s, c), align_bytes=256)
+                xq[(s, c)] = const.tile([P, NROWS * ROW], U32, name="xq%d%d" % (s, c), align_bytes=64)
+                xs[(s, c)] = const.tile([P, NROWS * ROW], U8, name="xs%d%d" % (s, c), align_bytes=64)
         ab = [const.tile([P, ROW, 28], F32, name="ab%d" % h) for h in range(2)]
 
         raws = {}
@@ -90,13 +90,8 @@ def tile_kernel_generated_1_t_kernel(tc, x, w1, w2, out):
             dst = w2g[c][:].rearrange("p (q i t) -> p q t i", i=4, t=4)
             nc.vector.tensor_copy(out=dst[:, 0:96], in_=src[:, 0:96])
             nc.scalar.copy(out=dst[:, 96:192], in_=src[:, 96:192])
-            for u in range(6):
-                wa = 48 + c * 768 + u * 128
-                sa = (c * 6 + u) * 256
-                nc.vector.quantize_mx(
-                    out=wq[:, wa:wa + 128].bitcast(FP8X4), scales=ws[:, sa:sa + 128],
-                    in_=w2g[c][:, u * 512:(u + 1) * 512],
-                )
+            nc.vector.quantize_mx(out=wq[:, c, 0:512].bitcast(FP8X4), scales=ws[:, c, 0:512], in_=w2g[c][:, 0:2048])
+            nc.vector.quantize_mx(out=wq[:, c, 512:768].bitcast(FP8X4), scales=ws[:, c, 512:768], in_=w2g[c][:, 2048:3072])
 
         def regroup(copy, g, c, mm, b0, b1):
             src = raws[(g, c, mm)][:].rearrange("p (t l b i) -> p b l t i", t=4, l=28, b=7, i=4)
@@ -132,8 +127,8 @@ def tile_kernel_generated_1_t_kernel(tc, x, w1, w2, out):
                 a = (n0 + k) * ROW
                 nc.tensor.matmul_mx(
                     out=ps[:, 0:width],
-                    lhsT=wq[:, 48 + c * 768 + col:48 + c * 768 + col + 128].bitcast(FP8X4),
-                    lhsT_scale=ws[:, (c * 6 + col // 128) * 256:(c * 6 + col // 128) * 256 + 128],
+                    lhsT=wq[:, c, col:col + 128].bitcast(FP8X4),
+                    lhsT_scale=ws[:, c, col:col + 128],
                     rhs=xq[key][:, a:a + width].bitcast(FP8X4),
                     rhs_scale=xs[key][:, a:a + width],
                     start=(c == 0 and k == 0),
@@ -168,37 +163,50 @@ def tile_kernel_generated_1_t_kernel(tc, x, w1, w2, out):
         vcopy = nc.vector.tensor_copy
         scopy = nc.scalar.copy
 
-        for c in range(2):
-            prep_w2(c)
-            for mm in range(2):
-                regroup(vcopy, 0, c, mm, 0, 4 - c)
-                regroup(scopy, 0, c, mm, 4 - c, 7)
-            quant_all(0, c)
-        load_group(2)
+        def main():
+            for c in range(2):
+                prep_w2(c)
+                for mm in range(2):
+                    regroup(vcopy, 0, c, mm, 0, 4 - c)
+                    regroup(scopy, 0, c, mm, 4 - c, 7)
+                quant_all(0, c)
+            load_group(2)
 
-        for g in range(GROUPS):
-            nxt = g + 1 < GROUPS
-            if nxt:
-                regroup(vcopy, g + 1, 0, 0, 0, 7)
-                regroup(scopy, g + 1, 1, 0, 0, 4)
-                regroup(vcopy, g + 1, 0, 1, 0, 6)
-                regroup(scopy, g + 1, 0, 1, 6, 7)
-                regroup(scopy, g + 1, 1, 0, 4, 7)
-            for j in range(8):
-                passes(g, j, 0)
-            if nxt:
-                quant_all(g + 1, 0)
-            for j in range(8):
-                passes(g, j, 1)
-                epilogue(g, j)
-                if nxt and j == 1:
-                    regroup(scopy, g + 1, 1, 1, 0, 4)
-                if nxt and j == 4:
-                    regroup(scopy, g + 1, 1, 1, 4, 7)
-                    if g + 3 < GROUPS:
-                        load_group(g + 3)
-                if j == 3:
-                    finish(g, 0)
-                if nxt and j == 6:
-                    quant_all(g + 1, 1)
-            finish(g, 1)
+            for g in range(GROUPS):
+                n = g + 1
+                nxt = n < GROUPS
+                if g > 0:
+                    for r0, nr in BANKS[0:3]:
+                        quant(g, 1, r0, nr)
+                if nxt:
+                    regroup(scopy, n, 1, 0, 0, 4)
+                    regroup(vcopy, n, 0, 0, 0, 7)
+                    regroup(scopy, n, 0, 1, 6, 7)
+                    regroup(scopy, n, 1, 0, 4, 7)
+                    regroup(vcopy, n, 0, 1, 0, 6)
+                    regroup(scopy, n, 1, 1, 0, 4)
+                    if g == 0:
+                        load_x(3, 0, 0)
+                        load_x(3, 0, 1)
+                        load_x(3, 1, 0)
+                if g > 0:
+                    quant(g, 1, 24, 4)
+                for j in range(8):
+                    passes(g, j, 0)
+                for j in range(8):
+                    if nxt and j < 2:
+                        quant(n, 0, BANKS[j][0], BANKS[j][1])
+                    if nxt and j == 4:
+                        quant(n, 0, 16, 8)
+                        quant(n, 0, 24, 4)
+                        regroup(scopy, n, 1, 1, 4, 7)
+                        if g == 0:
+                            load_x(3, 1, 1)
+                    passes(g, j, 1)
+                    epilogue(g, j)
+                    if j == 3:
+                        finish(g, 0)
+                finish(g, 1)
+
+        with tc.manual_schedule():
+            main()

@@ -19,7 +19,9 @@ P = 128
 GROUPS = 4
 ROW = 64
 NROWS = 30
-BANKS = ((0, 8), (8, 8), (16, 8), (24, 4))
+QBLOCKS = ((0, 8), (8, 8), (16, 8), (24, 4))
+BANKS_FIRST = ((0, 4), (4, 8), (12, 8), (20, 8))
+BANKS_REST = ((0, 8), (8, 8), (16, 8), (24, 4))
 
 
 def tile_kernel_generated_1_t_kernel(tc, x, w1, w2, out):
@@ -109,14 +111,20 @@ def tile_kernel_generated_1_t_kernel(tc, x, w1, w2, out):
             )
 
         def quant_all(g, c):
-            for r0, nr in BANKS:
+            for r0, nr in QBLOCKS:
                 quant(g, c, r0, nr)
 
         banks = {}
 
-        def passes(g, j, c):
+        def where(g, j):
+            if g == 0:
+                h, nb = j % 2, j // 2
+                return h, nb, BANKS_FIRST[nb]
             h, nb = j // 4, j % 4
-            n0, nr = BANKS[nb]
+            return h, nb, BANKS_REST[nb]
+
+        def passes(g, j, c):
+            h, nb, (n0, nr) = where(g, j)
             if c == 0:
                 banks[(g, j)] = psum.tile([P, 512], F32, name="ps", tag="ps")
             ps = banks[(g, j)]
@@ -138,8 +146,7 @@ def tile_kernel_generated_1_t_kernel(tc, x, w1, w2, out):
         outs = {}
 
         def epilogue(g, j):
-            h, nb = j // 4, j % 4
-            n0, nr = BANKS[nb]
+            h, nb, (n0, nr) = where(g, j)
             if nb == 0:
                 outs[(g, h)] = outp.tile([P, ROW, 28], F32, name="ot", tag="ot")
             ot = outs[(g, h)]
@@ -153,8 +160,9 @@ def tile_kernel_generated_1_t_kernel(tc, x, w1, w2, out):
         def finish(g, h):
             ov = outs[(g, h)][:].rearrange("p (m s) n -> p m s n", s=32)
             av = ab[h][:].rearrange("p (m s) n -> p m s n", s=32)
-            nc.vector.tensor_tensor(out=ov[:, :, 1, :], in0=ov[:, :, 1, :], in1=av[:, :, 28, :], op=ALU.add)
-            nc.vector.tensor_copy(out=ov[:, :, 0, :], in_=ov[:, :, 28, :])
+            eng = nc.vector
+            eng.tensor_tensor(out=ov[:, :, 1, :], in0=ov[:, :, 1, :], in1=av[:, :, 28, :], op=ALU.add)
+            eng.tensor_copy(out=ov[:, :, 0, :], in_=ov[:, :, 28, :])
             nc.sync.dma_start(
                 out=out[2 * g:2 * g + 2, h * P:(h + 1) * P].rearrange("m p l n -> p m (l n)"),
                 in_=ov[:, :, 0:28, :].rearrange("p m s n -> p m (s n)"),
@@ -163,50 +171,51 @@ def tile_kernel_generated_1_t_kernel(tc, x, w1, w2, out):
         vcopy = nc.vector.tensor_copy
         scopy = nc.scalar.copy
 
-        def main():
-            for c in range(2):
-                prep_w2(c)
-                for mm in range(2):
-                    regroup(vcopy, 0, c, mm, 0, 4 - c)
-                    regroup(scopy, 0, c, mm, 4 - c, 7)
-                quant_all(0, c)
-            load_group(2)
+        prep_w2(0)
+        regroup(vcopy, 0, 0, 0, 0, 2)
+        regroup(scopy, 0, 0, 0, 2, 4)
+        regroup(vcopy, 0, 0, 0, 4, 6)
+        regroup(scopy, 0, 0, 0, 6, 7)
+        regroup(vcopy, 0, 0, 1, 0, 2)
+        regroup(scopy, 0, 0, 1, 2, 4)
+        quant(0, 0, 0, 8)
+        regroup(vcopy, 0, 0, 1, 4, 6)
+        regroup(scopy, 0, 0, 1, 6, 7)
+        quant(0, 0, 8, 8)
+        quant(0, 0, 16, 8)
+        quant(0, 0, 24, 4)
+        prep_w2(1)
+        for mm in range(2):
+            regroup(vcopy, 0, 1, mm, 0, 3)
+            regroup(scopy, 0, 1, mm, 3, 7)
+        quant_all(0, 1)
+        load_group(2)
 
-            for g in range(GROUPS):
-                n = g + 1
-                nxt = n < GROUPS
-                if g > 0:
-                    for r0, nr in BANKS[0:3]:
-                        quant(g, 1, r0, nr)
-                if nxt:
-                    regroup(scopy, n, 1, 0, 0, 4)
-                    regroup(vcopy, n, 0, 0, 0, 7)
-                    regroup(scopy, n, 0, 1, 6, 7)
-                    regroup(scopy, n, 1, 0, 4, 7)
-                    regroup(vcopy, n, 0, 1, 0, 6)
-                    regroup(scopy, n, 1, 1, 0, 4)
-                    if g == 0:
-                        load_x(3, 0, 0)
-                        load_x(3, 0, 1)
-                        load_x(3, 1, 0)
-                if g > 0:
-                    quant(g, 1, 24, 4)
-                for j in range(8):
-                    passes(g, j, 0)
-                for j in range(8):
-                    if nxt and j < 2:
-                        quant(n, 0, BANKS[j][0], BANKS[j][1])
-                    if nxt and j == 4:
-                        quant(n, 0, 16, 8)
-                        quant(n, 0, 24, 4)
-                        regroup(scopy, n, 1, 1, 4, 7)
-                        if g == 0:
-                            load_x(3, 1, 1)
-                    passes(g, j, 1)
-                    epilogue(g, j)
-                    if j == 3:
-                        finish(g, 0)
-                finish(g, 1)
-
-        with tc.manual_schedule():
-            main()
+        for g in range(GROUPS):
+            nxt = g + 1 < GROUPS
+            if nxt:
+                regroup(vcopy, g + 1, 0, 0, 0, 7)
+                regroup(scopy, g + 1, 1, 0, 0, 4)
+                regroup(vcopy, g + 1, 0, 1, 0, 6)
+                regroup(scopy, g + 1, 0, 1, 6, 7)
+                regroup(scopy, g + 1, 1, 0, 4, 7)
+            for j in range(8):
+                passes(g, j, 0)
+            if nxt:
+                quant_all(g + 1, 0)
+            for j in range(8):
+                passes(g, j, 1)
+                epilogue(g, j)
+                if nxt and j == 1:
+                    regroup(scopy, g + 1, 1, 1, 0, 4)
+                if nxt and j == 4:
+                    regroup(scopy, g + 1, 1, 1, 4, 7)
+                    if g + 3 < GROUPS:
+                        load_group(g + 3)
+                if j == 3 and g > 0:
+                    finish(g, 0)
+                if nxt and j == 6:
+                    quant_all(g + 1, 1)
+            if g == 0:
+                finish(g, 0)
+            finish(g, 1)

@@ -16,71 +16,91 @@ FLOPS = 2 * M * L * H * J * K * I
 BYTES = 2 * M * J * L * H + 2 * J * K * I + 2 * I * 2 + 4 * M * I * L * H
 
 P = 128
-GROUPS = 4
 ROW = 64
-NROWS = 30
-QBLOCKS = ((0, 8), (8, 8), (16, 8), (24, 4))
-BANKS_FIRST = ((0, 4), (4, 8), (12, 8), (20, 8))
-BANKS_REST = ((0, 8), (8, 8), (16, 8), (24, 4))
+GROUPS = ((0, 32), (32, 64), (96, 64), (160, 64))
+NG = 4
+FULL_BANKS = ((0, 8), (8, 8), (16, 8), (24, 4))
+HALF_BANKS = ((0, 8), (8, 8))
+FULL_Q = ((0, 8), (8, 8), (16, 8), (24, 4))
+HALF_Q = ((0, 8), (8, 8), (16, 2))
+SPLIT = 16
+
+
+def segments(g):
+    f0, ns = GROUPS[g]
+    segs = []
+    for m in range(M):
+        a = max(f0, 28 * m)
+        b = min(f0 + ns, 28 * m + 28)
+        if b > a:
+            segs.append((m, a - 28 * m, b - 28 * m, a - f0))
+    return segs
 
 
 def tile_kernel_generated_1_t_kernel(tc, x, w1, w2, out):
     nc = tc.nc
     with ExitStack() as ctx:
         const = ctx.enter_context(tc.tile_pool(name="const", bufs=1))
-        rawp = ctx.enter_context(tc.tile_pool(name="rawp", bufs=8))
+        rawp = ctx.enter_context(tc.tile_pool(name="rawp", bufs=4))
+        gtp = ctx.enter_context(tc.tile_pool(name="gtp", bufs=4))
         outp = ctx.enter_context(tc.tile_pool(name="outp", bufs=4))
         psum = ctx.enter_context(tc.psum_pool(name="psum", bufs=8))
 
         w1b = const.tile([P, 2, 2], BF16, name="w1b")
         w1f = const.tile([P, 2, 2], F32, name="w1f")
-        w2raw = [const.tile([P, 3072], BF16, name="w2raw%d" % c) for c in range(2)]
-        w2g = [const.tile([P, 3072], BF16, name="w2g%d" % c, align_bytes=64) for c in range(2)]
         wq = const.tile([P, 2, 768], U32, name="wq", align_bytes=64)
         ws = const.tile([P, 2, 768], U8, name="ws", align_bytes=64)
-        gt = {}
         xq = {}
         xs = {}
         for s in range(2):
             for c in range(2):
-                gt[(s, c)] = const.tile([P, 28 * ROW * 4], BF16, name="gt%d%d" % (s, c), align_bytes=64)
-                xq[(s, c)] = const.tile([P, NROWS * ROW], U32, name="xq%d%d" % (s, c), align_bytes=64)
-                xs[(s, c)] = const.tile([P, NROWS * ROW], U8, name="xs%d%d" % (s, c), align_bytes=64)
-        ab = [const.tile([P, ROW, 28], F32, name="ab%d" % h) for h in range(2)]
+                xq[(s, c)] = const.tile([P, 30 * ROW], U32, name="xq%d%d" % (s, c), align_bytes=64)
+                xs[(s, c)] = const.tile([P, 30 * ROW], U8, name="xs%d%d" % (s, c), align_bytes=64)
+        ab = [const.tile([P, ROW + 1, 28], F32, name="ab%d" % h) for h in range(2)]
+        xx = [const.tile([P, M, 28], F32, name="xx%d" % h) for h in range(2)]
 
         raws = {}
+        gts = {}
+
+        w2raw = rawp.tile([P, 2, 3072], BF16, name="w2raw", tag="raw")
+        rawh = rawp.tile([P, 2, 4, 32 * 28], BF16, name="rawh", tag="raw")
 
         def load_w2(c):
             nc.sync.dma_start(
-                out=w2raw[c][:],
+                out=w2raw[:, c, :],
                 in_=w2[c * 512:(c + 1) * 512].rearrange("(p t) k i -> p (t k i)", p=P),
             )
 
-        def load_x(g, c, mm):
-            raw = rawp.tile([P, 3136], BF16, name="raw", tag="raw")
-            nc.sync.dma_start(
-                out=raw[:],
-                in_=x[2 * g + mm, c * 14336:(c + 1) * 14336, :].rearrange("(p r) n -> p (r n)", p=P),
-            )
-            raws[(g, c, mm)] = raw
-
-        def load_group(g):
-            for c in range(2):
-                for mm in range(2):
-                    load_x(g, c, mm)
+        def load_x(g, c):
+            if g == 0:
+                dst = rawh[:, c]
+            else:
+                raw = rawp.tile([P, 4, ROW * 28], BF16, name="raw", tag="raw")
+                raws[(g, c)] = raw
+                dst = raw[:]
+            for m, l0, l1, fl in segments(g):
+                nc.sync.dma_start(
+                    out=dst[:, :, fl * 28:(fl + l1 - l0) * 28],
+                    in_=x[m, c * 14336:(c + 1) * 14336, :].rearrange(
+                        "(p t l) n -> p t (l n)", p=P, t=4)[:, :, l0 * 28:l1 * 28],
+                )
 
         nc.scalar.dma_start(out=w1b[:], in_=w1.rearrange("(h p) s -> p h s", p=P))
         load_w2(0)
-        load_x(0, 0, 0)
-        load_x(0, 0, 1)
+        load_x(0, 0)
         load_w2(1)
-        load_x(0, 1, 0)
-        load_x(0, 1, 1)
-        load_group(1)
+        load_x(0, 1)
+        load_x(1, 0)
+        load_x(1, 1)
 
-        for key in sorted(gt):
-            nc.vector.memset(gt[key][:].rearrange("p (r s) -> p r s", s=128)[:, :, 112:128], 0.0)
-            for r in (0, NROWS - 1):
+        w2g = gtp.tile([P, 2, 3072], BF16, name="w2g", tag="gt", align_bytes=64)
+        for c in range(2):
+            gth = gtp.tile([P, 18 * ROW * 4], BF16, name="gth", tag="gt", align_bytes=64)
+            gts[(0, c)] = gth
+            nc.vector.memset(gth[:, 0:128], 0.0)
+            nc.vector.memset(gth[:, 13 * 256:18 * 256].rearrange("p (r q) -> p r q", q=256)[:, :, 128:256], 0.0)
+        for key in sorted(xq):
+            for r in (0, 29):
                 nc.vector.memset(xq[key][:, r * ROW:(r + 1) * ROW].bitcast(I32), 0)
                 nc.vector.memset(xs[key][:, r * ROW:(r + 1) * ROW].bitcast(I32), 0)
         for h in range(2):
@@ -88,17 +108,28 @@ def tile_kernel_generated_1_t_kernel(tc, x, w1, w2, out):
         nc.vector.tensor_copy(out=w1f[:], in_=w1b[:])
 
         def prep_w2(c):
-            src = w2raw[c][:].rearrange("p (t q i) -> p q t i", t=4, i=4)
-            dst = w2g[c][:].rearrange("p (q i t) -> p q t i", i=4, t=4)
+            src = w2raw[:, c, :].rearrange("p (t q i) -> p q t i", t=4, i=4)
+            dst = w2g[:, c, :].rearrange("p (q i t) -> p q t i", i=4, t=4)
             nc.vector.tensor_copy(out=dst[:, 0:96], in_=src[:, 0:96])
             nc.scalar.copy(out=dst[:, 96:192], in_=src[:, 96:192])
-            nc.vector.quantize_mx(out=wq[:, c, 0:512].bitcast(FP8X4), scales=ws[:, c, 0:512], in_=w2g[c][:, 0:2048])
-            nc.vector.quantize_mx(out=wq[:, c, 512:768].bitcast(FP8X4), scales=ws[:, c, 512:768], in_=w2g[c][:, 2048:3072])
+            nc.vector.quantize_mx(out=wq[:, c, 0:512].bitcast(FP8X4), scales=ws[:, c, 0:512], in_=w2g[:, c, 0:2048])
+            nc.vector.quantize_mx(out=wq[:, c, 512:768].bitcast(FP8X4), scales=ws[:, c, 512:768], in_=w2g[:, c, 2048:3072])
 
-        def regroup(copy, g, c, mm, b0, b1):
-            src = raws[(g, c, mm)][:].rearrange("p (t l b i) -> p b l t i", t=4, l=28, b=7, i=4)
-            dst = gt[(g % 2, c)][:].rearrange("p (b i m s t) -> p m b s t i", b=7, i=4, m=2, s=32, t=4)
-            copy(out=dst[:, mm, b0:b1, 0:28, :, :], in_=src[:, b0:b1])
+        def regroup(copy, g, c, b0, b1):
+            src = raws[(g, c)][:].rearrange("p t (f b i) -> p b f t i", b=7, i=4)
+            dst = gts[(g, c)][:].rearrange("p (b i f t) -> p b f t i", b=7, i=4, f=ROW, t=4)
+            copy(out=dst[:, b0:b1], in_=src[:, b0:b1])
+
+        def regroup_half(copy, c, hb, b0, b1):
+            src = rawh[:, c].rearrange("p t (f b i) -> p b f t i", b=7, i=4)
+            dst = gts[(0, c)][:, 256:256 + 4096].rearrange(
+                "p (b i e f t) -> p e b f t i", b=4, i=4, e=2, f=32, t=4)
+            copy(out=dst[:, hb, b0:b1], in_=src[:, 4 * hb + b0:4 * hb + b1])
+
+        def halo_half(copy, c, row, lane, n):
+            src = rawh[:, c].rearrange("p t (f n) -> p n f t", n=28)
+            a = (row * ROW + lane) * 4
+            copy(out=gts[(0, c)][:, a:a + 128].rearrange("p (f t) -> p f t", t=4), in_=src[:, n])
 
         def quant(g, c, r0, nr):
             key = (g % 2, c)
@@ -107,21 +138,22 @@ def tile_kernel_generated_1_t_kernel(tc, x, w1, w2, out):
             nc.vector.quantize_mx(
                 out=xq[key][:, a:b].bitcast(FP8X4),
                 scales=xs[key][:, a:b],
-                in_=gt[key][:, r0 * ROW * 4:(r0 + nr) * ROW * 4],
+                in_=gts[(g, c)][:, r0 * ROW * 4:(r0 + nr) * ROW * 4],
             )
 
         def quant_all(g, c):
-            for r0, nr in QBLOCKS:
+            for r0, nr in FULL_Q:
                 quant(g, c, r0, nr)
 
         banks = {}
 
+        def nbanks(g):
+            return 4 if g == 0 else 8
+
         def where(g, j):
             if g == 0:
-                h, nb = j % 2, j // 2
-                return h, nb, BANKS_FIRST[nb]
-            h, nb = j // 4, j % 4
-            return h, nb, BANKS_REST[nb]
+                return j % 2, j // 2, HALF_BANKS[j // 2]
+            return j // 4, j % 4, FULL_BANKS[j % 4]
 
         def passes(g, j, c):
             h, nb, (n0, nr) = where(g, j)
@@ -130,9 +162,10 @@ def tile_kernel_generated_1_t_kernel(tc, x, w1, w2, out):
             ps = banks[(g, j)]
             key = (g % 2, c)
             width = nr * ROW
+            shift = 1 if g == 0 else 0
             for k in range(K):
                 col = k * 256 + h * 128
-                a = (n0 + k) * ROW
+                a = (n0 + k + shift) * ROW
                 nc.tensor.matmul_mx(
                     out=ps[:, 0:width],
                     lhsT=wq[:, c, col:col + 128].bitcast(FP8X4),
@@ -145,76 +178,99 @@ def tile_kernel_generated_1_t_kernel(tc, x, w1, w2, out):
 
         outs = {}
 
+        def combine(h, ot, t4, ns, n0, nr):
+            nc.scalar.activation(out=ab[h][:, 1:ns + 1, n0:n0 + nr], in_=t4, func=ACT.Copy, scale=w1f[:, h, 1:2])
+            nc.vector.scalar_tensor_tensor(
+                out=ot[:, 0:ns, n0:n0 + nr], in0=t4, scalar=w1f[:, h, 0:1],
+                in1=ab[h][:, 0:ns, n0:n0 + nr], op0=ALU.mult, op1=ALU.add,
+            )
+
         def epilogue(g, j):
             h, nb, (n0, nr) = where(g, j)
             if nb == 0:
                 outs[(g, h)] = outp.tile([P, ROW, 28], F32, name="ot", tag="ot")
             ot = outs[(g, h)]
-            t4 = banks[(g, j)][:, 0:nr * ROW].rearrange("p (n f) -> p f n", f=ROW)[:, 0:60, :]
-            nc.scalar.activation(out=ab[h][:, 1:61, n0:n0 + nr], in_=t4, func=ACT.Copy, scale=w1f[:, h, 1:2])
-            nc.vector.scalar_tensor_tensor(
-                out=ot[:, 1:61, n0:n0 + nr], in0=t4, scalar=w1f[:, h, 0:1],
-                in1=ab[h][:, 0:60, n0:n0 + nr], op0=ALU.mult, op1=ALU.add,
-            )
+            ps = banks[(g, j)]
+            if g == 0:
+                t4 = ps[:, 0:512].rearrange("p (r e f) -> p e f r", e=2, f=32)
+                combine(h, ot, t4[:, 0], 32, n0, 8)
+                rest = min(8, 28 - SPLIT - n0)
+                combine(h, ot, t4[:, 1, :, 0:rest], 32, SPLIT + n0, rest)
+            else:
+                combine(h, ot, ps[:, 0:nr * ROW].rearrange("p (n f) -> p f n", f=ROW), ROW, n0, nr)
 
         def finish(g, h):
-            ov = outs[(g, h)][:].rearrange("p (m s) n -> p m s n", s=32)
-            av = ab[h][:].rearrange("p (m s) n -> p m s n", s=32)
-            eng = nc.vector
-            eng.tensor_tensor(out=ov[:, :, 1, :], in0=ov[:, :, 1, :], in1=av[:, :, 28, :], op=ALU.add)
-            eng.tensor_copy(out=ov[:, :, 0, :], in_=ov[:, :, 28, :])
-            nc.sync.dma_start(
-                out=out[2 * g:2 * g + 2, h * P:(h + 1) * P].rearrange("m p l n -> p m (l n)"),
-                in_=ov[:, :, 0:28, :].rearrange("p m s n -> p m (s n)"),
-            )
+            f0, ns = GROUPS[g]
+            ot = outs[(g, h)]
+            rows = slice(h * P, (h + 1) * P)
+            first = [m for m in range(M) if f0 <= 28 * m < f0 + ns]
+            last = [m for m in range(M) if f0 <= 28 * m + 27 < f0 + ns]
+            if first:
+                a = 28 * first[0] - f0
+                sl = slice(a, a + 28 * (len(first) - 1) + 1, 28)
+                nc.vector.tensor_tensor(out=xx[h][:, first[0]:first[-1] + 1, :], in0=ot[:, sl, :],
+                                        in1=ab[h][:, sl, :], op=ALU.subtract)
+            if last:
+                a = 28 * last[0] + 27 - f0
+                ms = slice(last[0], last[-1] + 1)
+                nc.vector.tensor_tensor(out=xx[h][:, ms, :], in0=xx[h][:, ms, :],
+                                        in1=ab[h][:, slice(a + 1, a + 28 * (len(last) - 1) + 2, 28), :], op=ALU.add)
+            for m, l0, l1, fl in segments(g):
+                la = max(l0, 1)
+                lb = min(l1, 27)
+                if lb > la:
+                    nc.sync.dma_start(
+                        out=out[m, rows, la + 1:lb + 1, :].rearrange("p l n -> p (l n)"),
+                        in_=ot[:, fl + la - l0:fl + lb - l0, :].rearrange("p s n -> p (s n)"),
+                    )
+            if last:
+                nc.sync.dma_start(out=out[ms, rows, 0, :].rearrange("m p n -> p m n"),
+                                  in_=ot[:, slice(a, a + 28 * (len(last) - 1) + 1, 28), :])
+                nc.sync.dma_start(out=out[ms, rows, 1, :].rearrange("m p n -> p m n"), in_=xx[h][:, ms, :])
+            if g + 1 < NG:
+                nc.gpsimd.tensor_copy(out=ab[h][:, 0, :], in_=ab[h][:, ns, :])
 
         vcopy = nc.vector.tensor_copy
         scopy = nc.scalar.copy
 
-        prep_w2(0)
-        regroup(vcopy, 0, 0, 0, 0, 2)
-        regroup(scopy, 0, 0, 0, 2, 4)
-        regroup(vcopy, 0, 0, 0, 4, 6)
-        regroup(scopy, 0, 0, 0, 6, 7)
-        regroup(vcopy, 0, 0, 1, 0, 2)
-        regroup(scopy, 0, 0, 1, 2, 4)
-        quant(0, 0, 0, 8)
-        regroup(vcopy, 0, 0, 1, 4, 6)
-        regroup(scopy, 0, 0, 1, 6, 7)
-        quant(0, 0, 8, 8)
-        quant(0, 0, 16, 8)
-        quant(0, 0, 24, 4)
-        prep_w2(1)
-        for mm in range(2):
-            regroup(vcopy, 0, 1, mm, 0, 3)
-            regroup(scopy, 0, 1, mm, 3, 7)
-        quant_all(0, 1)
-        load_group(2)
+        for c in range(2):
+            prep_w2(c)
+            regroup_half(vcopy, c, 0, 0, 2)
+            regroup_half(scopy, c, 1, 0, 2)
+            halo_half(vcopy, c, 0, 32, SPLIT - 1)
+            quant(0, c, 0, 8)
+            regroup_half(vcopy, c, 0, 2, 4)
+            regroup_half(scopy, c, 1, 2, 3)
+            halo_half(vcopy, c, 17, 0, SPLIT)
+            quant(0, c, 8, 8)
+            quant(0, c, 16, 2)
 
-        for g in range(GROUPS):
-            nxt = g + 1 < GROUPS
+        for g in range(NG):
+            nxt = g + 1 < NG
+            n = nbanks(g)
+            hooks = {}
             if nxt:
-                regroup(vcopy, g + 1, 0, 0, 0, 7)
-                regroup(scopy, g + 1, 1, 0, 0, 4)
-                regroup(vcopy, g + 1, 0, 1, 0, 6)
-                regroup(scopy, g + 1, 0, 1, 6, 7)
-                regroup(scopy, g + 1, 1, 0, 4, 7)
-            for j in range(8):
+                for c in range(2):
+                    gts[(g + 1, c)] = gtp.tile([P, 28 * ROW * 4], BF16, name="gt", tag="gt", align_bytes=64)
+                regroup(vcopy, g + 1, 0, 0, 6)
+                regroup(scopy, g + 1, 0, 6, 7)
+                regroup(scopy, g + 1, 1, 0, 2)
+                hooks = {n // 8: (2, 4), (3 * n) // 8: (4, 6), (5 * n) // 8: (6, 7)}
+            for j in range(n):
                 passes(g, j, 0)
             if nxt:
                 quant_all(g + 1, 0)
-            for j in range(8):
+            for j in range(n):
                 passes(g, j, 1)
                 epilogue(g, j)
-                if nxt and j == 1:
-                    regroup(scopy, g + 1, 1, 1, 0, 4)
-                if nxt and j == 4:
-                    regroup(scopy, g + 1, 1, 1, 4, 7)
-                    if g + 3 < GROUPS:
-                        load_group(g + 3)
-                if j == 3 and g > 0:
+                if j in hooks:
+                    regroup(scopy, g + 1, 1, hooks[j][0], hooks[j][1])
+                if j == n // 2 and g + 2 < NG:
+                    load_x(g + 2, 0)
+                    load_x(g + 2, 1)
+                if g > 0 and j == 3:
                     finish(g, 0)
-                if nxt and j == 6:
+                if nxt and j == (3 * n) // 4:
                     quant_all(g + 1, 1)
             if g == 0:
                 finish(g, 0)

@@ -41,9 +41,8 @@ def tile_kernel_generated_1_t_kernel(tc, x, w1, w2, out):
     nc = tc.nc
     with ExitStack() as ctx:
         const = ctx.enter_context(tc.tile_pool(name="const", bufs=1))
-        rawp = ctx.enter_context(tc.tile_pool(name="rawp", bufs=4))
+        rawp = ctx.enter_context(tc.tile_pool(name="rawp", bufs=8))
         gtp = ctx.enter_context(tc.tile_pool(name="gtp", bufs=4))
-        outp = ctx.enter_context(tc.tile_pool(name="outp", bufs=4))
         psum = ctx.enter_context(tc.psum_pool(name="psum", bufs=8))
 
         w1b = const.tile([P, 2, 2], BF16, name="w1b")
@@ -57,40 +56,46 @@ def tile_kernel_generated_1_t_kernel(tc, x, w1, w2, out):
                 xq[(s, c)] = const.tile([P, 30 * ROW], U32, name="xq%d%d" % (s, c), align_bytes=64)
                 xs[(s, c)] = const.tile([P, 30 * ROW], U8, name="xs%d%d" % (s, c), align_bytes=64)
         ab = [const.tile([P, ROW + 1, 28], F32, name="ab%d" % h) for h in range(2)]
-        xx = [const.tile([P, M, 28], F32, name="xx%d" % h) for h in range(2)]
+        ot = [const.tile([P, M * 28 + 1, 28], F32, name="ot%d" % h) for h in range(2)]
 
         raws = {}
         gts = {}
 
-        w2raw = rawp.tile([P, 2, 3072], BF16, name="w2raw", tag="raw")
-        rawh = rawp.tile([P, 2, 4, 32 * 28], BF16, name="rawh", tag="raw")
+        w2raw = {}
+        rawh = {}
 
         def load_w2(c):
+            w2raw[c] = rawp.tile([P, 3072], BF16, name="w2raw", tag="raw")
             nc.sync.dma_start(
-                out=w2raw[:, c, :],
+                out=w2raw[c][:],
                 in_=w2[c * 512:(c + 1) * 512].rearrange("(p t) k i -> p (t k i)", p=P),
             )
 
-        def load_x(g, c):
-            if g == 0:
-                dst = rawh[:, c]
-            else:
-                raw = rawp.tile([P, 4, ROW * 28], BF16, name="raw", tag="raw")
-                raws[(g, c)] = raw
-                dst = raw[:]
-            for m, l0, l1, fl in segments(g):
+        def load_half(c):
+            rawh[c] = rawp.tile([P, 4, 32 * 28], BF16, name="rawh", tag="raw")
+            for m, l0, l1, fl in segments(0):
                 nc.sync.dma_start(
-                    out=dst[:, :, fl * 28:(fl + l1 - l0) * 28],
+                    out=rawh[c][:, :, fl * 28:(fl + l1 - l0) * 28],
                     in_=x[m, c * 14336:(c + 1) * 14336, :].rearrange(
                         "(p t l) n -> p t (l n)", p=P, t=4)[:, :, l0 * 28:l1 * 28],
                 )
 
+        def load_x(m, c):
+            raw = rawp.tile([P, 3136], BF16, name="raw", tag="raw")
+            nc.sync.dma_start(
+                out=raw[:],
+                in_=x[m, c * 14336:(c + 1) * 14336, :].rearrange("(p r) n -> p (r n)", p=P),
+            )
+            raws[(m, c)] = raw
+
         nc.scalar.dma_start(out=w1b[:], in_=w1.rearrange("(h p) s -> p h s", p=P))
         load_w2(0)
-        load_x(0, 0)
+        load_half(0)
         load_w2(1)
-        load_x(0, 1)
+        load_half(1)
         load_x(1, 0)
+        load_x(2, 0)
+        load_x(3, 0)
         load_x(1, 1)
 
         w2g = gtp.tile([P, 2, 3072], BF16, name="w2g", tag="gt", align_bytes=64)
@@ -108,26 +113,27 @@ def tile_kernel_generated_1_t_kernel(tc, x, w1, w2, out):
         nc.vector.tensor_copy(out=w1f[:], in_=w1b[:])
 
         def prep_w2(c):
-            src = w2raw[:, c, :].rearrange("p (t q i) -> p q t i", t=4, i=4)
+            src = w2raw[c][:].rearrange("p (t q i) -> p q t i", t=4, i=4)
             dst = w2g[:, c, :].rearrange("p (q i t) -> p q t i", i=4, t=4)
             nc.vector.tensor_copy(out=dst[:, 0:96], in_=src[:, 0:96])
             nc.scalar.copy(out=dst[:, 96:192], in_=src[:, 96:192])
             nc.vector.quantize_mx(out=wq[:, c, 0:512].bitcast(FP8X4), scales=ws[:, c, 0:512], in_=w2g[:, c, 0:2048])
             nc.vector.quantize_mx(out=wq[:, c, 512:768].bitcast(FP8X4), scales=ws[:, c, 512:768], in_=w2g[:, c, 2048:3072])
 
-        def regroup(copy, g, c, b0, b1):
-            src = raws[(g, c)][:].rearrange("p t (f b i) -> p b f t i", b=7, i=4)
+        def regroup(copy, g, c, s, b0, b1):
+            m, l0, l1, fl = segments(g)[s]
+            src = raws[(m, c)][:].rearrange("p (t l b i) -> p b l t i", t=4, l=28, b=7, i=4)
             dst = gts[(g, c)][:].rearrange("p (b i f t) -> p b f t i", b=7, i=4, f=ROW, t=4)
-            copy(out=dst[:, b0:b1], in_=src[:, b0:b1])
+            copy(out=dst[:, b0:b1, fl:fl + l1 - l0], in_=src[:, b0:b1, l0:l1])
 
         def regroup_half(copy, c, hb, b0, b1):
-            src = rawh[:, c].rearrange("p t (f b i) -> p b f t i", b=7, i=4)
+            src = rawh[c][:].rearrange("p t (f b i) -> p b f t i", b=7, i=4)
             dst = gts[(0, c)][:, 256:256 + 4096].rearrange(
                 "p (b i e f t) -> p e b f t i", b=4, i=4, e=2, f=32, t=4)
             copy(out=dst[:, hb, b0:b1], in_=src[:, 4 * hb + b0:4 * hb + b1])
 
         def halo_half(copy, c, row, lane, n):
-            src = rawh[:, c].rearrange("p t (f n) -> p n f t", n=28)
+            src = rawh[c][:].rearrange("p t (f n) -> p n f t", n=28)
             a = (row * ROW + lane) * 4
             copy(out=gts[(0, c)][:, a:a + 128].rearrange("p (f t) -> p f t", t=4), in_=src[:, n])
 
@@ -176,57 +182,43 @@ def tile_kernel_generated_1_t_kernel(tc, x, w1, w2, out):
                     stop=(c == 1 and k == K - 1),
                 )
 
-        outs = {}
-
-        def combine(h, ot, t4, ns, n0, nr):
+        def combine(h, f0, t4, ns, n0, nr):
             nc.scalar.activation(out=ab[h][:, 1:ns + 1, n0:n0 + nr], in_=t4, func=ACT.Copy, scale=w1f[:, h, 1:2])
             nc.vector.scalar_tensor_tensor(
-                out=ot[:, 0:ns, n0:n0 + nr], in0=t4, scalar=w1f[:, h, 0:1],
+                out=ot[h][:, f0 + 1:f0 + ns + 1, n0:n0 + nr], in0=t4, scalar=w1f[:, h, 0:1],
                 in1=ab[h][:, 0:ns, n0:n0 + nr], op0=ALU.mult, op1=ALU.add,
             )
 
         def epilogue(g, j):
             h, nb, (n0, nr) = where(g, j)
-            if nb == 0:
-                outs[(g, h)] = outp.tile([P, ROW, 28], F32, name="ot", tag="ot")
-            ot = outs[(g, h)]
+            f0 = GROUPS[g][0]
             ps = banks[(g, j)]
             if g == 0:
                 t4 = ps[:, 0:512].rearrange("p (r e f) -> p e f r", e=2, f=32)
-                combine(h, ot, t4[:, 0], 32, n0, 8)
+                combine(h, f0, t4[:, 0], 32, n0, 8)
                 rest = min(8, 28 - SPLIT - n0)
-                combine(h, ot, t4[:, 1, :, 0:rest], 32, SPLIT + n0, rest)
+                combine(h, f0, t4[:, 1, :, 0:rest], 32, SPLIT + n0, rest)
             else:
-                combine(h, ot, ps[:, 0:nr * ROW].rearrange("p (n f) -> p f n", f=ROW), ROW, n0, nr)
+                combine(h, f0, ps[:, 0:nr * ROW].rearrange("p (n f) -> p f n", f=ROW), ROW, n0, nr)
 
         def finish(g, h):
             f0, ns = GROUPS[g]
-            ot = outs[(g, h)]
-            rows = slice(h * P, (h + 1) * P)
             first = [m for m in range(M) if f0 <= 28 * m < f0 + ns]
             last = [m for m in range(M) if f0 <= 28 * m + 27 < f0 + ns]
+            eng = nc.gpsimd if g + 1 < NG else nc.vector
             if first:
-                a = 28 * first[0] - f0
-                sl = slice(a, a + 28 * (len(first) - 1) + 1, 28)
-                nc.vector.tensor_tensor(out=xx[h][:, first[0]:first[-1] + 1, :], in0=ot[:, sl, :],
-                                        in1=ab[h][:, sl, :], op=ALU.subtract)
-            if last:
-                a = 28 * last[0] + 27 - f0
-                ms = slice(last[0], last[-1] + 1)
-                nc.vector.tensor_tensor(out=xx[h][:, ms, :], in0=xx[h][:, ms, :],
-                                        in1=ab[h][:, slice(a + 1, a + 28 * (len(last) - 1) + 2, 28), :], op=ALU.add)
-            for m, l0, l1, fl in segments(g):
-                la = max(l0, 1)
-                lb = min(l1, 27)
-                if lb > la:
-                    nc.sync.dma_start(
-                        out=out[m, rows, la + 1:lb + 1, :].rearrange("p l n -> p (l n)"),
-                        in_=ot[:, fl + la - l0:fl + lb - l0, :].rearrange("p s n -> p (s n)"),
-                    )
-            if last:
-                nc.sync.dma_start(out=out[ms, rows, 0, :].rearrange("m p n -> p m n"),
-                                  in_=ot[:, slice(a, a + 28 * (len(last) - 1) + 1, 28), :])
-                nc.sync.dma_start(out=out[ms, rows, 1, :].rearrange("m p n -> p m n"), in_=xx[h][:, ms, :])
+                o = slice(28 * first[0] + 1, 28 * first[-1] + 2, 28)
+                a = slice(28 * first[0] - f0, 28 * first[-1] - f0 + 1, 28)
+                eng.tensor_tensor(out=ot[h][:, o, :], in0=ot[h][:, o, :], in1=ab[h][:, a, :], op=ALU.subtract)
+            o = slice(28 * last[0] + 1, 28 * last[-1] + 2, 28)
+            a = slice(28 * last[0] + 28 - f0, 28 * last[-1] + 29 - f0, 28)
+            eng.tensor_tensor(out=ot[h][:, o, :], in0=ot[h][:, o, :], in1=ab[h][:, a, :], op=ALU.add)
+            for m in last:
+                eng.tensor_copy(out=ot[h][:, 28 * m, :], in_=ot[h][:, 28 * m + 28, :])
+            nc.sync.dma_start(
+                out=out[last[0]:last[-1] + 1, h * P:(h + 1) * P].rearrange("m p l n -> p m (l n)"),
+                in_=ot[h][:, 28 * last[0]:28 * last[-1] + 28, :].rearrange("p (m s) n -> p m (s n)", s=28),
+            )
             if g + 1 < NG:
                 nc.gpsimd.tensor_copy(out=ab[h][:, 0, :], in_=ab[h][:, ns, :])
 
@@ -245,29 +237,42 @@ def tile_kernel_generated_1_t_kernel(tc, x, w1, w2, out):
             quant(0, c, 8, 8)
             quant(0, c, 16, 2)
 
+        load_x(2, 1)
+        load_x(3, 1)
+        load_x(4, 0)
+        load_x(5, 0)
+        later = {0: ((4, 1), (5, 1)), 1: ((6, 0), (7, 0), (6, 1), (7, 1))}
+
         for g in range(NG):
             nxt = g + 1 < NG
             n = nbanks(g)
-            hooks = {}
+            hooks = []
             if nxt:
                 for c in range(2):
                     gts[(g + 1, c)] = gtp.tile([P, 28 * ROW * 4], BF16, name="gt", tag="gt", align_bytes=64)
-                regroup(vcopy, g + 1, 0, 0, 6)
-                regroup(scopy, g + 1, 0, 6, 7)
-                regroup(scopy, g + 1, 1, 0, 2)
-                hooks = {n // 8: (2, 4), (3 * n) // 8: (4, 6), (5 * n) // 8: (6, 7)}
+                whole = 2 if g + 1 == NG - 1 else 1
+                parts = [s for s in range(3) if s != whole]
+                regroup(vcopy, g + 1, 0, whole, 0, 6)
+                regroup(scopy, g + 1, 0, parts[0], 0, 7)
+                regroup(vcopy, g + 1, 0, whole, 6, 7)
+                regroup(scopy, g + 1, 0, parts[1], 0, 7)
+                hooks = [(0, parts[0], 0, 4), (n // 4, parts[0], 4, 7),
+                         (n // 2, parts[1], 0, 4), ((5 * n) // 8, parts[1], 4, 7)]
             for j in range(n):
                 passes(g, j, 0)
             if nxt:
                 quant_all(g + 1, 0)
+                regroup(vcopy, g + 1, 1, whole, 0, 6)
+                regroup(vcopy, g + 1, 1, whole, 6, 7)
             for j in range(n):
                 passes(g, j, 1)
                 epilogue(g, j)
-                if j in hooks:
-                    regroup(scopy, g + 1, 1, hooks[j][0], hooks[j][1])
-                if j == n // 2 and g + 2 < NG:
-                    load_x(g + 2, 0)
-                    load_x(g + 2, 1)
+                for when, s, b0, b1 in hooks:
+                    if when == j:
+                        regroup(scopy, g + 1, 1, s, b0, b1)
+                if j == n // 2:
+                    for m, c in later.get(g, ()):
+                        load_x(m, c)
                 if g > 0 and j == 3:
                     finish(g, 0)
                 if nxt and j == (3 * n) // 4:

@@ -17,8 +17,10 @@ BYTES = 2 * M * J * L * H + 2 * J * K * I + 2 * I * 2 + 4 * M * I * L * H
 
 P = 128
 ROW = 64
-GROUPS = ((0, 32), (32, 64), (96, 64), (160, 64))
+GROUPS = ((0, 64), (64, 64), (128, 64), (192, 32))
 NG = 4
+LASTG = NG - 1
+FIRST_BANKS = ((0, 4), (4, 8), (12, 8), (20, 8))
 FULL_BANKS = ((0, 8), (8, 8), (16, 8), (24, 4))
 HALF_BANKS = ((0, 8), (8, 8))
 FULL_Q = ((0, 8), (8, 8), (16, 8), (24, 4))
@@ -60,20 +62,20 @@ def tile_kernel_generated_1_t_kernel(tc, x, w1, w2, out):
 
         raws = {}
         gts = {}
-
         w2raw = {}
         rawh = {}
 
-        def load_w2(c):
-            w2raw[c] = rawp.tile([P, 3072], BF16, name="w2raw", tag="raw")
-            nc.sync.dma_start(
-                out=w2raw[c][:],
-                in_=w2[c * 512:(c + 1) * 512].rearrange("(p t) k i -> p (t k i)", p=P),
-            )
+        def load_w2(c, pieces):
+            w2raw[c] = rawp.tile([P, 4, 768], BF16, name="w2raw", tag="raw")
+            for k0, k1 in pieces:
+                nc.sync.dma_start(
+                    out=w2raw[c][:, :, k0 * 256:k1 * 256],
+                    in_=w2[c * 512:(c + 1) * 512, k0:k1, :].rearrange("(p t) k i -> p t (k i)", p=P),
+                )
 
         def load_half(c):
             rawh[c] = rawp.tile([P, 4, 32 * 28], BF16, name="rawh", tag="raw")
-            for m, l0, l1, fl in segments(0):
+            for m, l0, l1, fl in segments(LASTG):
                 nc.sync.dma_start(
                     out=rawh[c][:, :, fl * 28:(fl + l1 - l0) * 28],
                     in_=x[m, c * 14336:(c + 1) * 14336, :].rearrange(
@@ -89,21 +91,14 @@ def tile_kernel_generated_1_t_kernel(tc, x, w1, w2, out):
             raws[(m, c)] = raw
 
         nc.scalar.dma_start(out=w1b[:], in_=w1.rearrange("(h p) s -> p h s", p=P))
-        load_w2(0)
-        load_half(0)
-        load_w2(1)
-        load_half(1)
-        load_x(1, 0)
-        load_x(2, 0)
-        load_x(3, 0)
-        load_x(1, 1)
+        load_w2(0, ((0, 1), (1, 3)))
+        for m in range(3):
+            load_x(m, 0)
+        load_w2(1, ((0, 3),))
+        for m in range(3):
+            load_x(m, 1)
 
         w2g = gtp.tile([P, 2, 3072], BF16, name="w2g", tag="gt", align_bytes=64)
-        for c in range(2):
-            gth = gtp.tile([P, 18 * ROW * 4], BF16, name="gth", tag="gt", align_bytes=64)
-            gts[(0, c)] = gth
-            nc.vector.memset(gth[:, 0:128], 0.0)
-            nc.vector.memset(gth[:, 13 * 256:18 * 256].rearrange("p (r q) -> p r q", q=256)[:, :, 128:256], 0.0)
         for key in sorted(xq):
             for r in (0, 29):
                 nc.vector.memset(xq[key][:, r * ROW:(r + 1) * ROW].bitcast(I32), 0)
@@ -112,13 +107,14 @@ def tile_kernel_generated_1_t_kernel(tc, x, w1, w2, out):
             nc.vector.memset(ab[h][:, 0, :], 0.0)
         nc.vector.tensor_copy(out=w1f[:], in_=w1b[:])
 
-        def prep_w2(c):
-            src = w2raw[c][:].rearrange("p (t q i) -> p q t i", t=4, i=4)
+        def regroup_w2(copy, c, q0, q1):
+            src = w2raw[c][:].rearrange("p t (q i) -> p q t i", i=4)
             dst = w2g[:, c, :].rearrange("p (q i t) -> p q t i", i=4, t=4)
-            nc.vector.tensor_copy(out=dst[:, 0:96], in_=src[:, 0:96])
-            nc.scalar.copy(out=dst[:, 96:192], in_=src[:, 96:192])
-            nc.vector.quantize_mx(out=wq[:, c, 0:512].bitcast(FP8X4), scales=ws[:, c, 0:512], in_=w2g[:, c, 0:2048])
-            nc.vector.quantize_mx(out=wq[:, c, 512:768].bitcast(FP8X4), scales=ws[:, c, 512:768], in_=w2g[:, c, 2048:3072])
+            copy(out=dst[:, q0:q1], in_=src[:, q0:q1])
+
+        def quant_w2(c, c0, c1):
+            nc.vector.quantize_mx(out=wq[:, c, c0:c1].bitcast(FP8X4), scales=ws[:, c, c0:c1],
+                                  in_=w2g[:, c, 4 * c0:4 * c1])
 
         def regroup(copy, g, c, s, b0, b1):
             m, l0, l1, fl = segments(g)[s]
@@ -128,14 +124,14 @@ def tile_kernel_generated_1_t_kernel(tc, x, w1, w2, out):
 
         def regroup_half(copy, c, hb, b0, b1):
             src = rawh[c][:].rearrange("p t (f b i) -> p b f t i", b=7, i=4)
-            dst = gts[(0, c)][:, 256:256 + 4096].rearrange(
+            dst = gts[(LASTG, c)][:, 256:256 + 4096].rearrange(
                 "p (b i e f t) -> p e b f t i", b=4, i=4, e=2, f=32, t=4)
             copy(out=dst[:, hb, b0:b1], in_=src[:, 4 * hb + b0:4 * hb + b1])
 
         def halo_half(copy, c, row, lane, n):
             src = rawh[c][:].rearrange("p t (f n) -> p n f t", n=28)
             a = (row * ROW + lane) * 4
-            copy(out=gts[(0, c)][:, a:a + 128].rearrange("p (f t) -> p f t", t=4), in_=src[:, n])
+            copy(out=gts[(LASTG, c)][:, a:a + 128].rearrange("p (f t) -> p f t", t=4), in_=src[:, n])
 
         def quant(g, c, r0, nr):
             key = (g % 2, c)
@@ -148,17 +144,19 @@ def tile_kernel_generated_1_t_kernel(tc, x, w1, w2, out):
             )
 
         def quant_all(g, c):
-            for r0, nr in FULL_Q:
+            for r0, nr in (HALF_Q if g == LASTG else FULL_Q):
                 quant(g, c, r0, nr)
 
         banks = {}
 
         def nbanks(g):
-            return 4 if g == 0 else 8
+            return 4 if g == LASTG else 8
 
         def where(g, j):
             if g == 0:
-                return j % 2, j // 2, HALF_BANKS[j // 2]
+                return j % 2, j // 2, FIRST_BANKS[j // 2]
+            if g == LASTG:
+                return j // 2, j % 2, HALF_BANKS[j % 2]
             return j // 4, j % 4, FULL_BANKS[j % 4]
 
         def passes(g, j, c):
@@ -168,7 +166,7 @@ def tile_kernel_generated_1_t_kernel(tc, x, w1, w2, out):
             ps = banks[(g, j)]
             key = (g % 2, c)
             width = nr * ROW
-            shift = 1 if g == 0 else 0
+            shift = 1 if g == LASTG else 0
             for k in range(K):
                 col = k * 256 + h * 128
                 a = (n0 + k + shift) * ROW
@@ -193,7 +191,7 @@ def tile_kernel_generated_1_t_kernel(tc, x, w1, w2, out):
             h, nb, (n0, nr) = where(g, j)
             f0 = GROUPS[g][0]
             ps = banks[(g, j)]
-            if g == 0:
+            if g == LASTG:
                 t4 = ps[:, 0:512].rearrange("p (r e f) -> p e f r", e=2, f=32)
                 combine(h, f0, t4[:, 0], 32, n0, 8)
                 rest = min(8, 28 - SPLIT - n0)
@@ -201,82 +199,119 @@ def tile_kernel_generated_1_t_kernel(tc, x, w1, w2, out):
             else:
                 combine(h, f0, ps[:, 0:nr * ROW].rearrange("p (n f) -> p f n", f=ROW), ROW, n0, nr)
 
+        def store(h, m, r0, r1):
+            nc.sync.dma_start(
+                out=out[m, h * P:(h + 1) * P, r0:r1, :].rearrange("p l n -> p (l n)"),
+                in_=ot[h][:, 28 * m + r0:28 * m + r1, :].rearrange("p s n -> p (s n)"),
+            )
+
+        EARLY = 24
+
         def finish(g, h):
             f0, ns = GROUPS[g]
             first = [m for m in range(M) if f0 <= 28 * m < f0 + ns]
             last = [m for m in range(M) if f0 <= 28 * m + 27 < f0 + ns]
-            eng = nc.gpsimd if g + 1 < NG else nc.vector
-            if first:
-                o = slice(28 * first[0] + 1, 28 * first[-1] + 2, 28)
-                a = slice(28 * first[0] - f0, 28 * first[-1] - f0 + 1, 28)
-                eng.tensor_tensor(out=ot[h][:, o, :], in0=ot[h][:, o, :], in1=ab[h][:, a, :], op=ALU.subtract)
+            eng = nc.gpsimd if g < LASTG else nc.vector
+            o = slice(28 * first[0] + 1, 28 * first[-1] + 2, 28)
+            a = slice(28 * first[0] - f0, 28 * first[-1] - f0 + 1, 28)
+            eng.tensor_tensor(out=ot[h][:, o, :], in0=ot[h][:, o, :], in1=ab[h][:, a, :], op=ALU.subtract)
             o = slice(28 * last[0] + 1, 28 * last[-1] + 2, 28)
             a = slice(28 * last[0] + 28 - f0, 28 * last[-1] + 29 - f0, 28)
             eng.tensor_tensor(out=ot[h][:, o, :], in0=ot[h][:, o, :], in1=ab[h][:, a, :], op=ALU.add)
             for m in last:
                 eng.tensor_copy(out=ot[h][:, 28 * m, :], in_=ot[h][:, 28 * m + 28, :])
-            nc.sync.dma_start(
-                out=out[last[0]:last[-1] + 1, h * P:(h + 1) * P].rearrange("m p l n -> p m (l n)"),
-                in_=ot[h][:, 28 * last[0]:28 * last[-1] + 28, :].rearrange("p (m s) n -> p m (s n)", s=28),
-            )
-            if g + 1 < NG:
+            if g < LASTG:
+                nc.sync.dma_start(
+                    out=out[last[0]:last[-1] + 1, h * P:(h + 1) * P].rearrange("m p l n -> p m (l n)"),
+                    in_=ot[h][:, 28 * last[0]:28 * last[-1] + 28, :].rearrange("p (m s) n -> p m (s n)", s=28),
+                )
                 nc.gpsimd.tensor_copy(out=ab[h][:, 0, :], in_=ab[h][:, ns, :])
+            else:
+                store(h, last[1], 0, 28)
+                store(h, last[0], EARLY, 28)
+                store(h, last[0], 0, 2)
+            if g == LASTG - 1:
+                store(h, last[-1] + 1, 2, EARLY)
 
         vcopy = nc.vector.tensor_copy
         scopy = nc.scalar.copy
 
         for c in range(2):
-            prep_w2(c)
-            regroup_half(vcopy, c, 0, 0, 2)
-            regroup_half(scopy, c, 1, 0, 2)
-            halo_half(vcopy, c, 0, 32, SPLIT - 1)
-            quant(0, c, 0, 8)
-            regroup_half(vcopy, c, 0, 2, 4)
-            regroup_half(scopy, c, 1, 2, 3)
-            halo_half(vcopy, c, 17, 0, SPLIT)
-            quant(0, c, 8, 8)
-            quant(0, c, 16, 2)
+            gts[(0, c)] = gtp.tile([P, 28 * ROW * 4], BF16, name="gt", tag="gt", align_bytes=64)
+        regroup_w2(vcopy, 0, 0, 64)
+        quant_w2(0, 0, 256)
+        for s in range(2):
+            regroup(vcopy, 0, 0, s, 0, 2)
+            regroup(scopy, 0, 0, s, 2, 4)
+            regroup(vcopy, 0, 0, s, 4, 6)
+            regroup(scopy, 0, 0, s, 6, 7)
+        regroup_w2(scopy, 0, 64, 128)
+        regroup_w2(vcopy, 0, 128, 192)
+        quant_w2(0, 256, 768)
+        regroup(vcopy, 0, 0, 2, 0, 2)
+        regroup(scopy, 0, 0, 2, 2, 7)
+        quant_all(0, 0)
+        regroup_w2(vcopy, 1, 0, 96)
+        regroup_w2(scopy, 1, 96, 192)
+        quant_w2(1, 0, 512)
+        quant_w2(1, 512, 768)
+        for s in range(2):
+            regroup(vcopy, 0, 1, s, 0, 2)
+            regroup(vcopy, 0, 1, s, 2, 3)
+            regroup(scopy, 0, 1, s, 3, 7)
+        regroup(vcopy, 0, 1, 2, 0, 2)
+        regroup(scopy, 0, 1, 2, 2, 7)
+        quant_all(0, 1)
 
-        load_x(2, 1)
-        load_x(3, 1)
-        load_x(4, 0)
-        load_x(5, 0)
-        later = {0: ((4, 1), (5, 1)), 1: ((6, 0), (7, 0), (6, 1), (7, 1))}
+        for m, c in ((3, 0), (4, 0), (3, 1), (4, 1), (5, 0), (6, 0), (5, 1), (6, 1)):
+            load_x(m, c)
+        load_half(0)
+        load_half(1)
 
         for g in range(NG):
-            nxt = g + 1 < NG
+            nxt = g + 1
             n = nbanks(g)
             hooks = []
-            if nxt:
+            if nxt < LASTG:
                 for c in range(2):
-                    gts[(g + 1, c)] = gtp.tile([P, 28 * ROW * 4], BF16, name="gt", tag="gt", align_bytes=64)
-                whole = 2 if g + 1 == NG - 1 else 1
-                parts = [s for s in range(3) if s != whole]
-                regroup(vcopy, g + 1, 0, whole, 0, 6)
-                regroup(scopy, g + 1, 0, parts[0], 0, 7)
-                regroup(vcopy, g + 1, 0, whole, 6, 7)
-                regroup(scopy, g + 1, 0, parts[1], 0, 7)
-                hooks = [(0, parts[0], 0, 4), (n // 4, parts[0], 4, 7),
-                         (n // 2, parts[1], 0, 4), ((5 * n) // 8, parts[1], 4, 7)]
+                    gts[(nxt, c)] = gtp.tile([P, 28 * ROW * 4], BF16, name="gt", tag="gt", align_bytes=64)
+                regroup(vcopy, nxt, 0, 1, 0, 6)
+                regroup(scopy, nxt, 0, 0, 0, 7)
+                regroup(vcopy, nxt, 0, 1, 6, 7)
+                regroup(scopy, nxt, 0, 2, 0, 7)
+                hooks = [(0, 0, 0, 4), (n // 4, 0, 4, 7), (n // 2, 2, 0, 4), ((5 * n) // 8, 2, 4, 7)]
+            if nxt == LASTG:
+                for c in range(2):
+                    gth = gtp.tile([P, 18 * ROW * 4], BF16, name="gth", tag="gt", align_bytes=64)
+                    gts[(nxt, c)] = gth
+                    nc.gpsimd.memset(gth[:, 0:128], 0.0)
+                    nc.gpsimd.memset(gth[:, 13 * 256:18 * 256].rearrange("p (r q) -> p r q", q=256)[:, :, 128:256], 0.0)
+                regroup_half(vcopy, 0, 0, 0, 4)
+                regroup_half(scopy, 0, 1, 0, 3)
+                halo_half(vcopy, 0, 0, 32, SPLIT - 1)
+                halo_half(vcopy, 0, 17, 0, SPLIT)
             for j in range(n):
                 passes(g, j, 0)
-            if nxt:
-                quant_all(g + 1, 0)
-                regroup(vcopy, g + 1, 1, whole, 0, 6)
-                regroup(vcopy, g + 1, 1, whole, 6, 7)
+            if nxt < NG:
+                quant_all(nxt, 0)
+            if nxt < LASTG:
+                regroup(vcopy, nxt, 1, 1, 0, 6)
+                regroup(vcopy, nxt, 1, 1, 6, 7)
+            if nxt == LASTG:
+                regroup_half(vcopy, 1, 0, 0, 4)
+                regroup_half(scopy, 1, 1, 0, 3)
+                halo_half(vcopy, 1, 0, 32, SPLIT - 1)
+                halo_half(vcopy, 1, 17, 0, SPLIT)
             for j in range(n):
                 passes(g, j, 1)
                 epilogue(g, j)
                 for when, s, b0, b1 in hooks:
                     if when == j:
-                        regroup(scopy, g + 1, 1, s, b0, b1)
-                if j == n // 2:
-                    for m, c in later.get(g, ()):
-                        load_x(m, c)
-                if g > 0 and j == 3:
+                        regroup(scopy, nxt, 1, s, b0, b1)
+                if g > 0 and j == n // 2 - 1:
                     finish(g, 0)
-                if nxt and j == (3 * n) // 4:
-                    quant_all(g + 1, 1)
+                if nxt < NG and j == (3 * n) // 4:
+                    quant_all(nxt, 1)
             if g == 0:
                 finish(g, 0)
             finish(g, 1)

@@ -57,8 +57,8 @@ def tile_kernel_generated_1_t_kernel(tc, x, w1, w2, out):
             for c in range(2):
                 xq[(s, c)] = const.tile([P, 30 * ROW], U32, name="xq%d%d" % (s, c), align_bytes=64)
                 xs[(s, c)] = const.tile([P, 30 * ROW], U8, name="xs%d%d" % (s, c), align_bytes=64)
-        ab = [const.tile([P, ROW + 1, 28], F32, name="ab%d" % h) for h in range(2)]
-        ot = [const.tile([P, M * 28 + 1, 28], F32, name="ot%d" % h) for h in range(2)]
+        ab = const.tile([P, 2, ROW + 1, 28], F32, name="ab")
+        ot = const.tile([P, 2, M * 28 + 1, 28], F32, name="ot")
 
         raws = {}
         gts = {}
@@ -103,8 +103,7 @@ def tile_kernel_generated_1_t_kernel(tc, x, w1, w2, out):
             for r in (0, 29):
                 nc.vector.memset(xq[key][:, r * ROW:(r + 1) * ROW].bitcast(I32), 0)
                 nc.vector.memset(xs[key][:, r * ROW:(r + 1) * ROW].bitcast(I32), 0)
-        for h in range(2):
-            nc.vector.memset(ab[h][:, 0, :], 0.0)
+        nc.vector.memset(ab[:, :, 0, :], 0.0)
         nc.vector.tensor_copy(out=w1f[:], in_=w1b[:])
 
         def regroup_w2(copy, c, q0, q1):
@@ -181,10 +180,10 @@ def tile_kernel_generated_1_t_kernel(tc, x, w1, w2, out):
                 )
 
         def combine(h, f0, t4, ns, n0, nr):
-            nc.scalar.activation(out=ab[h][:, 1:ns + 1, n0:n0 + nr], in_=t4, func=ACT.Copy, scale=w1f[:, h, 1:2])
+            nc.scalar.activation(out=ab[:, h, 1:ns + 1, n0:n0 + nr], in_=t4, func=ACT.Copy, scale=w1f[:, h, 1:2])
             nc.vector.scalar_tensor_tensor(
-                out=ot[h][:, f0 + 1:f0 + ns + 1, n0:n0 + nr], in0=t4, scalar=w1f[:, h, 0:1],
-                in1=ab[h][:, 0:ns, n0:n0 + nr], op0=ALU.mult, op1=ALU.add,
+                out=ot[:, h, f0 + 1:f0 + ns + 1, n0:n0 + nr], in0=t4, scalar=w1f[:, h, 0:1],
+                in1=ab[:, h, 0:ns, n0:n0 + nr], op0=ALU.mult, op1=ALU.add,
             )
 
         def epilogue(g, j):
@@ -202,36 +201,37 @@ def tile_kernel_generated_1_t_kernel(tc, x, w1, w2, out):
         def store(h, m, r0, r1):
             nc.sync.dma_start(
                 out=out[m, h * P:(h + 1) * P, r0:r1, :].rearrange("p l n -> p (l n)"),
-                in_=ot[h][:, 28 * m + r0:28 * m + r1, :].rearrange("p s n -> p (s n)"),
+                in_=ot[:, h, 28 * m + r0:28 * m + r1, :].rearrange("p s n -> p (s n)"),
             )
 
         EARLY = 24
 
-        def finish(g, h):
+        def finish(g, hs):
             f0, ns = GROUPS[g]
             first = [m for m in range(M) if f0 <= 28 * m < f0 + ns]
             last = [m for m in range(M) if f0 <= 28 * m + 27 < f0 + ns]
-            eng = nc.gpsimd if g < LASTG else nc.vector
             o = slice(28 * first[0] + 1, 28 * first[-1] + 2, 28)
             a = slice(28 * first[0] - f0, 28 * first[-1] - f0 + 1, 28)
-            eng.tensor_tensor(out=ot[h][:, o, :], in0=ot[h][:, o, :], in1=ab[h][:, a, :], op=ALU.subtract)
+            nc.vector.tensor_tensor(out=ot[:, hs, o, :], in0=ot[:, hs, o, :], in1=ab[:, hs, a, :], op=ALU.subtract)
             o = slice(28 * last[0] + 1, 28 * last[-1] + 2, 28)
             a = slice(28 * last[0] + 28 - f0, 28 * last[-1] + 29 - f0, 28)
-            eng.tensor_tensor(out=ot[h][:, o, :], in0=ot[h][:, o, :], in1=ab[h][:, a, :], op=ALU.add)
+            nc.vector.tensor_tensor(out=ot[:, hs, o, :], in0=ot[:, hs, o, :], in1=ab[:, hs, a, :], op=ALU.add)
             for m in last:
-                eng.tensor_copy(out=ot[h][:, 28 * m, :], in_=ot[h][:, 28 * m + 28, :])
+                nc.scalar.copy(out=ot[:, hs, 28 * m, :], in_=ot[:, hs, 28 * m + 28, :])
+            for h in range(hs.start, hs.stop):
+                if g < LASTG:
+                    nc.sync.dma_start(
+                        out=out[last[0]:last[-1] + 1, h * P:(h + 1) * P].rearrange("m p l n -> p m (l n)"),
+                        in_=ot[:, h, 28 * last[0]:28 * last[-1] + 28, :].rearrange("p (m s) n -> p m (s n)", s=28),
+                    )
+                else:
+                    store(h, last[1], 0, 28)
+                    store(h, last[0], EARLY, 28)
+                    store(h, last[0], 0, 2)
+                if g == LASTG - 1:
+                    store(h, last[-1] + 1, 2, EARLY)
             if g < LASTG:
-                nc.sync.dma_start(
-                    out=out[last[0]:last[-1] + 1, h * P:(h + 1) * P].rearrange("m p l n -> p m (l n)"),
-                    in_=ot[h][:, 28 * last[0]:28 * last[-1] + 28, :].rearrange("p (m s) n -> p m (s n)", s=28),
-                )
-                nc.gpsimd.tensor_copy(out=ab[h][:, 0, :], in_=ab[h][:, ns, :])
-            else:
-                store(h, last[1], 0, 28)
-                store(h, last[0], EARLY, 28)
-                store(h, last[0], 0, 2)
-            if g == LASTG - 1:
-                store(h, last[-1] + 1, 2, EARLY)
+                nc.scalar.copy(out=ab[:, hs, 0, :], in_=ab[:, hs, ns, :])
 
         vcopy = nc.vector.tensor_copy
         scopy = nc.scalar.copy
@@ -284,8 +284,8 @@ def tile_kernel_generated_1_t_kernel(tc, x, w1, w2, out):
                 for c in range(2):
                     gth = gtp.tile([P, 18 * ROW * 4], BF16, name="gth", tag="gt", align_bytes=64)
                     gts[(nxt, c)] = gth
-                    nc.gpsimd.memset(gth[:, 0:128], 0.0)
-                    nc.gpsimd.memset(gth[:, 13 * 256:18 * 256].rearrange("p (r q) -> p r q", q=256)[:, :, 128:256], 0.0)
+                    nc.vector.memset(gth[:, 0:128], 0.0)
+                    nc.vector.memset(gth[:, 13 * 256:18 * 256].rearrange("p (r q) -> p r q", q=256)[:, :, 128:256], 0.0)
                 regroup_half(vcopy, 0, 0, 0, 4)
                 regroup_half(scopy, 0, 1, 0, 3)
                 halo_half(vcopy, 0, 0, 32, SPLIT - 1)
@@ -308,10 +308,8 @@ def tile_kernel_generated_1_t_kernel(tc, x, w1, w2, out):
                 for when, s, b0, b1 in hooks:
                     if when == j:
                         regroup(scopy, nxt, 1, s, b0, b1)
-                if g > 0 and j == n // 2 - 1:
-                    finish(g, 0)
+                if g == LASTG and j == n // 2 - 1:
+                    finish(g, slice(0, 1))
                 if nxt < NG and j == (3 * n) // 4:
                     quant_all(nxt, 1)
-            if g == 0:
-                finish(g, 0)
-            finish(g, 1)
+            finish(g, slice(1, 2) if g == LASTG else slice(0, 2))

@@ -22,10 +22,10 @@ NG = 4
 LASTG = NG - 1
 FIRST_BANKS = ((0, 4), (4, 8), (12, 8), (20, 8))
 FULL_BANKS = ((0, 8), (8, 8), (16, 8), (24, 4))
-HALF_BANKS = ((0, 8), (8, 8))
+HALF_BANKS = ((0, 8), (8, 4), (12, 2))
 FULL_Q = ((0, 8), (8, 8), (16, 8), (24, 4))
-HALF_Q = ((0, 8), (8, 8), (16, 2))
-SPLIT = 16
+HALF_Q = ((0, 8), (8, 8))
+SPLIT = 14
 
 
 def segments(g):
@@ -58,7 +58,8 @@ def tile_kernel_generated_1_t_kernel(tc, x, w1, w2, out):
                 xq[(s, c)] = const.tile([P, 30 * ROW], U32, name="xq%d%d" % (s, c), align_bytes=64)
                 xs[(s, c)] = const.tile([P, 30 * ROW], U8, name="xs%d%d" % (s, c), align_bytes=64)
         ab = const.tile([P, 2, ROW + 1, 28], F32, name="ab")
-        ot = const.tile([P, 2, M * 28 + 1, 28], F32, name="ot")
+        ot = const.tile([P, 2, (M + 1) * 28, 28], F32, name="ot")
+        xx = const.tile([P, 2, M, 28], F32, name="xx")
 
         raws = {}
         gts = {}
@@ -121,16 +122,16 @@ def tile_kernel_generated_1_t_kernel(tc, x, w1, w2, out):
             dst = gts[(g, c)][:].rearrange("p (b i f t) -> p b f t i", b=7, i=4, f=ROW, t=4)
             copy(out=dst[:, b0:b1, fl:fl + l1 - l0], in_=src[:, b0:b1, l0:l1])
 
-        def regroup_half(copy, c, hb, b0, b1):
-            src = rawh[c][:].rearrange("p t (f b i) -> p b f t i", b=7, i=4)
-            dst = gts[(LASTG, c)][:, 256:256 + 4096].rearrange(
-                "p (b i e f t) -> p e b f t i", b=4, i=4, e=2, f=32, t=4)
-            copy(out=dst[:, hb, b0:b1], in_=src[:, 4 * hb + b0:4 * hb + b1])
+        def regroup_half(copy, c, b0, b1):
+            src = rawh[c][:].rearrange("p t (u b i) -> p b u t i", b=7, i=2)
+            dst = gts[(LASTG, c)][:, 256:256 + SPLIT * 256].rearrange(
+                "p (b i u t) -> p b u t i", b=7, i=2, u=ROW, t=4)
+            copy(out=dst[:, b0:b1], in_=src[:, b0:b1])
 
-        def halo_half(copy, c, row, lane, n):
+        def halo_half(copy, c, row, e, n):
             src = rawh[c][:].rearrange("p t (f n) -> p n f t", n=28)
-            a = (row * ROW + lane) * 4
-            copy(out=gts[(LASTG, c)][:, a:a + 128].rearrange("p (f t) -> p f t", t=4), in_=src[:, n])
+            dst = gts[(LASTG, c)][:, row * 256:(row + 1) * 256].rearrange("p (f e t) -> p e f t", e=2, t=4)
+            copy(out=dst[:, e], in_=src[:, n])
 
         def quant(g, c, r0, nr):
             key = (g % 2, c)
@@ -149,13 +150,13 @@ def tile_kernel_generated_1_t_kernel(tc, x, w1, w2, out):
         banks = {}
 
         def nbanks(g):
-            return 4 if g == LASTG else 8
+            return 6 if g == LASTG else 8
 
         def where(g, j):
             if g == 0:
                 return j % 2, j // 2, FIRST_BANKS[j // 2]
             if g == LASTG:
-                return j // 2, j % 2, HALF_BANKS[j % 2]
+                return j // 3, j % 3, HALF_BANKS[j % 3]
             return j // 4, j % 4, FULL_BANKS[j % 4]
 
         def passes(g, j, c):
@@ -179,24 +180,26 @@ def tile_kernel_generated_1_t_kernel(tc, x, w1, w2, out):
                     stop=(c == 1 and k == K - 1),
                 )
 
-        def combine(h, f0, t4, ns, n0, nr):
-            nc.scalar.activation(out=ab[:, h, 1:ns + 1, n0:n0 + nr], in_=t4, func=ACT.Copy, scale=w1f[:, h, 1:2])
-            nc.vector.scalar_tensor_tensor(
-                out=ot[:, h, f0 + 1:f0 + ns + 1, n0:n0 + nr], in0=t4, scalar=w1f[:, h, 0:1],
-                in1=ab[:, h, 0:ns, n0:n0 + nr], op0=ALU.mult, op1=ALU.add,
-            )
+        def combine(h, t4, later, before, result):
+            nc.scalar.activation(out=later, in_=t4, func=ACT.Copy, scale=w1f[:, h, 1:2])
+            nc.vector.scalar_tensor_tensor(out=result, in0=t4, scalar=w1f[:, h, 0:1], in1=before,
+                                           op0=ALU.mult, op1=ALU.add)
+
+        def halves(ap, u0, n0, nr):
+            return ap.rearrange("p s n -> p (s n)").rearrange("p (u r) -> p u r", r=SPLIT)[:, u0:u0 + ROW, n0:n0 + nr]
 
         def epilogue(g, j):
             h, nb, (n0, nr) = where(g, j)
             f0 = GROUPS[g][0]
             ps = banks[(g, j)]
             if g == LASTG:
-                t4 = ps[:, 0:512].rearrange("p (r e f) -> p e f r", e=2, f=32)
-                combine(h, f0, t4[:, 0], 32, n0, 8)
-                rest = min(8, 28 - SPLIT - n0)
-                combine(h, f0, t4[:, 1, :, 0:rest], 32, SPLIT + n0, rest)
+                combine(h, ps[:, 0:nr * ROW].rearrange("p (r u) -> p u r", u=ROW),
+                        halves(ab[:, h], 2, n0, nr), halves(ab[:, h], 0, n0, nr),
+                        halves(ot[:, h], 2 * f0 + 2, n0, nr))
             else:
-                combine(h, f0, ps[:, 0:nr * ROW].rearrange("p (n f) -> p f n", f=ROW), ROW, n0, nr)
+                combine(h, ps[:, 0:nr * ROW].rearrange("p (n f) -> p f n", f=ROW),
+                        ab[:, h, 1:ROW + 1, n0:n0 + nr], ab[:, h, 0:ROW, n0:n0 + nr],
+                        ot[:, h, f0 + 1:f0 + ROW + 1, n0:n0 + nr])
 
         def store(h, m, r0, r1):
             nc.sync.dma_start(
@@ -206,30 +209,39 @@ def tile_kernel_generated_1_t_kernel(tc, x, w1, w2, out):
 
         EARLY = 24
 
+        def store_pair(h, m0, m1):
+            nc.sync.dma_start(
+                out=out[m0:m1 + 1, h * P:(h + 1) * P, 0:2, :].rearrange("m p l n -> p m (l n)"),
+                in_=ot[:, h, 28 * m0 + 28:28 * m1 + 56, :].rearrange(
+                    "p (m s) n -> p m s n", s=28)[:, :, 0:2, :].rearrange("p m s n -> p m (s n)"),
+            )
+
         def finish(g, hs):
             f0, ns = GROUPS[g]
             first = [m for m in range(M) if f0 <= 28 * m < f0 + ns]
             last = [m for m in range(M) if f0 <= 28 * m + 27 < f0 + ns]
-            o = slice(28 * first[0] + 1, 28 * first[-1] + 2, 28)
-            a = slice(28 * first[0] - f0, 28 * first[-1] - f0 + 1, 28)
-            nc.vector.tensor_tensor(out=ot[:, hs, o, :], in0=ot[:, hs, o, :], in1=ab[:, hs, a, :], op=ALU.subtract)
-            o = slice(28 * last[0] + 1, 28 * last[-1] + 2, 28)
-            a = slice(28 * last[0] + 28 - f0, 28 * last[-1] + 29 - f0, 28)
-            nc.vector.tensor_tensor(out=ot[:, hs, o, :], in0=ot[:, hs, o, :], in1=ab[:, hs, a, :], op=ALU.add)
-            for m in last:
-                nc.scalar.copy(out=ot[:, hs, 28 * m, :], in_=ot[:, hs, 28 * m + 28, :])
             for h in range(hs.start, hs.stop):
                 if g < LASTG:
                     nc.sync.dma_start(
-                        out=out[last[0]:last[-1] + 1, h * P:(h + 1) * P].rearrange("m p l n -> p m (l n)"),
-                        in_=ot[:, h, 28 * last[0]:28 * last[-1] + 28, :].rearrange("p (m s) n -> p m (s n)", s=28),
+                        out=out[last[0]:last[-1] + 1, h * P:(h + 1) * P, 2:28, :].rearrange("m p l n -> p m (l n)"),
+                        in_=ot[:, h, 28 * last[0]:28 * last[-1] + 28, :].rearrange(
+                            "p (m s) n -> p m s n", s=28)[:, :, 2:28, :].rearrange("p m s n -> p m (s n)"),
                     )
                 else:
-                    store(h, last[1], 0, 28)
+                    store(h, last[1], 2, 28)
                     store(h, last[0], EARLY, 28)
-                    store(h, last[0], 0, 2)
                 if g == LASTG - 1:
                     store(h, last[-1] + 1, 2, EARLY)
+            o = slice(28 * first[0] + 1, 28 * first[-1] + 2, 28)
+            a = slice(28 * first[0] - f0, 28 * first[-1] - f0 + 1, 28)
+            nc.vector.tensor_tensor(out=xx[:, hs, first[0]:first[-1] + 1, :], in0=ot[:, hs, o, :],
+                                    in1=ab[:, hs, a, :], op=ALU.subtract)
+            o = slice(28 * last[0] + 29, 28 * last[-1] + 30, 28)
+            a = slice(28 * last[0] + 28 - f0, 28 * last[-1] + 29 - f0, 28)
+            nc.vector.tensor_tensor(out=ot[:, hs, o, :], in0=xx[:, hs, last[0]:last[-1] + 1, :],
+                                    in1=ab[:, hs, a, :], op=ALU.add)
+            for h in range(hs.start, hs.stop):
+                store_pair(h, last[0], last[-1])
             if g < LASTG:
                 nc.scalar.copy(out=ab[:, hs, 0, :], in_=ab[:, hs, ns, :])
 
@@ -282,14 +294,15 @@ def tile_kernel_generated_1_t_kernel(tc, x, w1, w2, out):
                 hooks = [(0, 0, 0, 4), (n // 4, 0, 4, 7), (n // 2, 2, 0, 4), ((5 * n) // 8, 2, 4, 7)]
             if nxt == LASTG:
                 for c in range(2):
-                    gth = gtp.tile([P, 18 * ROW * 4], BF16, name="gth", tag="gt", align_bytes=64)
+                    gth = gtp.tile([P, (SPLIT + 2) * ROW * 4], BF16, name="gth", tag="gt", align_bytes=64)
                     gts[(nxt, c)] = gth
-                    nc.vector.memset(gth[:, 0:128], 0.0)
-                    nc.vector.memset(gth[:, 13 * 256:18 * 256].rearrange("p (r q) -> p r q", q=256)[:, :, 128:256], 0.0)
-                regroup_half(vcopy, 0, 0, 0, 4)
-                regroup_half(scopy, 0, 1, 0, 3)
-                halo_half(vcopy, 0, 0, 32, SPLIT - 1)
-                halo_half(vcopy, 0, 17, 0, SPLIT)
+                    nc.vector.memset(gth[:, 0:256], 0.0)
+                    nc.vector.memset(gth[:, (SPLIT + 1) * 256:(SPLIT + 2) * 256], 0.0)
+                regroup_half(vcopy, 0, 0, 2)
+                regroup_half(scopy, 0, 2, 4)
+                regroup_half(scopy, 0, 4, 7)
+                halo_half(vcopy, 0, 0, 1, SPLIT - 1)
+                halo_half(vcopy, 0, SPLIT + 1, 0, SPLIT)
             for j in range(n):
                 passes(g, j, 0)
             if nxt < NG:
@@ -298,10 +311,11 @@ def tile_kernel_generated_1_t_kernel(tc, x, w1, w2, out):
                 regroup(vcopy, nxt, 1, 1, 0, 6)
                 regroup(vcopy, nxt, 1, 1, 6, 7)
             if nxt == LASTG:
-                regroup_half(vcopy, 1, 0, 0, 4)
-                regroup_half(scopy, 1, 1, 0, 3)
-                halo_half(vcopy, 1, 0, 32, SPLIT - 1)
-                halo_half(vcopy, 1, 17, 0, SPLIT)
+                regroup_half(vcopy, 1, 0, 2)
+                regroup_half(scopy, 1, 2, 4)
+                regroup_half(scopy, 1, 4, 7)
+                halo_half(vcopy, 1, 0, 1, SPLIT - 1)
+                halo_half(vcopy, 1, SPLIT + 1, 0, SPLIT)
             for j in range(n):
                 passes(g, j, 1)
                 epilogue(g, j)

@@ -291,7 +291,7 @@ def tile_kernel_generated_1_t_kernel(tc, x, w1, w2, out):
                 regroup(scopy, nxt, 0, 0, 0, 7)
                 regroup(vcopy, nxt, 0, 1, 6, 7)
                 regroup(scopy, nxt, 0, 2, 0, 7)
-                hooks = [(0, 0, 0, 4), (n // 4, 0, 4, 7), (n // 2, 2, 0, 4), ((5 * n) // 8, 2, 4, 7)]
+                hooks = [(0, 0, 0, 4), (n // 4, 0, 4, 7), (n // 2, 2, 0, 4), ((5 * n) // 8, 2, 6, 7)]
             if nxt == LASTG:
                 for c in range(2):
                     gth = gtp.tile([P, (SPLIT + 2) * ROW * 4], BF16, name="gth", tag="gt", align_bytes=64)
@@ -310,6 +310,7 @@ def tile_kernel_generated_1_t_kernel(tc, x, w1, w2, out):
             if nxt < LASTG:
                 regroup(vcopy, nxt, 1, 1, 0, 6)
                 regroup(vcopy, nxt, 1, 1, 6, 7)
+                regroup(vcopy, nxt, 1, 2, 4, 6)
             if nxt == LASTG:
                 regroup_half(vcopy, 1, 0, 2)
                 regroup_half(scopy, 1, 2, 4)

@@ -24,7 +24,8 @@ FIRST_BANKS = ((0, 4), (4, 8), (12, 8), (20, 8))
 FULL_BANKS = ((0, 8), (8, 8), (16, 8), (24, 4))
 HALF_BANKS = ((0, 8), (8, 4), (12, 2))
 FULL_Q = ((0, 8), (8, 8), (16, 8), (24, 4))
-HALF_Q = ((0, 8), (8, 8))
+WIDE_Q = ((0, 16), (16, 8), (24, 4))
+HALF_Q = ((0, 16),)
 SPLIT = 14
 
 
@@ -144,7 +145,7 @@ def tile_kernel_generated_1_t_kernel(tc, x, w1, w2, out):
             )
 
         def quant_all(g, c):
-            for r0, nr in (HALF_Q if g == LASTG else FULL_Q):
+            for r0, nr in (HALF_Q if g == LASTG else FULL_Q if g == 0 else WIDE_Q):
                 quant(g, c, r0, nr)
 
         banks = {}

@@ -304,8 +304,9 @@ def tile_kernel_generated_1_t_kernel(tc, x, w1, w2, out):
                 regroup_half(scopy, 0, 4, 7)
                 halo_half(vcopy, 0, 0, 1, SPLIT - 1)
                 halo_half(vcopy, 0, SPLIT + 1, 0, SPLIT)
-            for j in range(n):
-                passes(g, j, 0)
+            if g == 0:
+                for j in range(n):
+                    passes(g, j, 0)
             if nxt < NG:
                 quant_all(nxt, 0)
             if nxt < LASTG:
@@ -319,6 +320,8 @@ def tile_kernel_generated_1_t_kernel(tc, x, w1, w2, out):
                 halo_half(vcopy, 1, 0, 1, SPLIT - 1)
                 halo_half(vcopy, 1, SPLIT + 1, 0, SPLIT)
             for j in range(n):
+                if g > 0:
+                    passes(g, j, 0)
                 passes(g, j, 1)
                 epilogue(g, j)
                 for when, s, b0, b1 in hooks:

from contextlib import ExitStack

import concourse.mybir as mybir

FP8X4 = mybir.dt.float8_e4m3fn_x4
BF16 = mybir.dt.bfloat16
F32 = mybir.dt.float32
U32 = mybir.dt.uint32
U8 = mybir.dt.uint8
I32 = mybir.dt.int32
ALU = mybir.AluOpType
ACT = mybir.ActivationFunctionType

M, J, L, H, K, I = 8, 1024, 28, 28, 3, 256
FLOPS = 2 * M * L * H * J * K * I
BYTES = 2 * M * J * L * H + 2 * J * K * I + 2 * I * 2 + 4 * M * I * L * H

P = 128
ROW = 64
GROUPS = ((0, 64), (64, 64), (128, 64), (192, 32))
NG = 4
LASTG = NG - 1
FIRST_BANKS = ((0, 4), (4, 8), (12, 8), (20, 8))
FULL_BANKS = ((0, 8), (8, 8), (16, 8), (24, 4))
HALF_BANKS = ((0, 8), (8, 4), (12, 2))
FULL_Q = ((0, 8), (8, 8), (16, 8), (24, 4))
WIDE_Q = ((0, 16), (16, 8), (24, 4))
HALF_Q = ((0, 16),)
SPLIT = 14


def segments(g):
    f0, ns = GROUPS[g]
    segs = []
    for m in range(M):
        a = max(f0, 28 * m)
        b = min(f0 + ns, 28 * m + 28)
        if b > a:
            segs.append((m, a - 28 * m, b - 28 * m, a - f0))
    return segs


def tile_kernel_generated_1_t_kernel(tc, x, w1, w2, out):
    nc = tc.nc
    with ExitStack() as ctx:
        const = ctx.enter_context(tc.tile_pool(name="const", bufs=1))
        rawp = ctx.enter_context(tc.tile_pool(name="rawp", bufs=8))
        gtp = ctx.enter_context(tc.tile_pool(name="gtp", bufs=4))
        psum = ctx.enter_context(tc.psum_pool(name="psum", bufs=8))

        w1b = const.tile([P, 2, 2], BF16, name="w1b")
        w1f = const.tile([P, 2, 2], F32, name="w1f")
        wq = const.tile([P, 2, 768], U32, name="wq", align_bytes=64)
        ws = const.tile([P, 2, 768], U8, name="ws", align_bytes=64)
        xq = {}
        xs = {}
        for s in range(2):
            for c in range(2):
                xq[(s, c)] = const.tile([P, 30 * ROW], U32, name="xq%d%d" % (s, c), align_bytes=64)
                xs[(s, c)] = const.tile([P, 30 * ROW], U8, name="xs%d%d" % (s, c), align_bytes=64)
        ab = const.tile([P, 2, ROW + 1, 28], F32, name="ab")
        ot = const.tile([P, 2, (M + 1) * 28, 28], F32, name="ot")
        xx = const.tile([P, 2, M, 28], F32, name="xx")

        raws = {}
        gts = {}
        w2raw = {}
        rawh = {}

        def load_w2(c, pieces):
            w2raw[c] = rawp.tile([P, 4, 768], BF16, name="w2raw", tag="raw")
            for k0, k1 in pieces:
                nc.sync.dma_start(
                    out=w2raw[c][:, :, k0 * 256:k1 * 256],
                    in_=w2[c * 512:(c + 1) * 512, k0:k1, :].rearrange("(p t) k i -> p t (k i)", p=P),
                )

        def load_half(c):
            rawh[c] = rawp.tile([P, 4, 32 * 28], BF16, name="rawh", tag="raw")
            for m, l0, l1, fl in segments(LASTG):
                nc.sync.dma_start(
                    out=rawh[c][:, :, fl * 28:(fl + l1 - l0) * 28],
                    in_=x[m, c * 14336:(c + 1) * 14336, :].rearrange(
                        "(p t l) n -> p t (l n)", p=P, t=4)[:, :, l0 * 28:l1 * 28],
                )

        def load_x(m, c):
            raw = rawp.tile([P, 3136], BF16, name="raw", tag="raw")
            nc.sync.dma_start(
                out=raw[:],
                in_=x[m, c * 14336:(c + 1) * 14336, :].rearrange("(p r) n -> p (r n)", p=P),
            )
            raws[(m, c)] = raw

        nc.scalar.dma_start(out=w1b[:], in_=w1.rearrange("(h p) s -> p h s", p=P))
        load_w2(0, ((0, 1), (1, 3)))
        for m in range(3):
            load_x(m, 0)
        load_w2(1, ((0, 3),))
        for m in range(3):
            load_x(m, 1)

        w2g = gtp.tile([P, 2, 3072], BF16, name="w2g", tag="gt", align_bytes=64)
        for key in sorted(xq):
            for r in (0, 29):
                nc.vector.memset(xq[key][:, r * ROW:(r + 1) * ROW].bitcast(I32), 0)
                nc.vector.memset(xs[key][:, r * ROW:(r + 1) * ROW].bitcast(I32), 0)
        nc.vector.memset(ab[:, :, 0, :], 0.0)
        nc.vector.tensor_copy(out=w1f[:], in_=w1b[:])

        def regroup_w2(copy, c, q0, q1):
            src = w2raw[c][:].rearrange("p t (q i) -> p q t i", i=4)
            dst = w2g[:, c, :].rearrange("p (q i t) -> p q t i", i=4, t=4)
            copy(out=dst[:, q0:q1], in_=src[:, q0:q1])

        def quant_w2(c, c0, c1):
            nc.vector.quantize_mx(out=wq[:, c, c0:c1].bitcast(FP8X4), scales=ws[:, c, c0:c1],
                                  in_=w2g[:, c, 4 * c0:4 * c1])

        def regroup(copy, g, c, s, b0, b1):
            m, l0, l1, fl = segments(g)[s]
            src = raws[(m, c)][:].rearrange("p (t l b i) -> p b l t i", t=4, l=28, b=7, i=4)
            dst = gts[(g, c)][:].rearrange("p (b i f t) -> p b f t i", b=7, i=4, f=ROW, t=4)
            copy(out=dst[:, b0:b1, fl:fl + l1 - l0], in_=src[:, b0:b1, l0:l1])

        def regroup_half(copy, c, b0, b1):
            src = rawh[c][:].rearrange("p t (u b i) -> p b u t i", b=7, i=2)
            dst = gts[(LASTG, c)][:, 256:256 + SPLIT * 256].rearrange(
                "p (b i u t) -> p b u t i", b=7, i=2, u=ROW, t=4)
            copy(out=dst[:, b0:b1], in_=src[:, b0:b1])

        def halo_half(copy, c, row, e, n):
            src = rawh[c][:].rearrange("p t (f n) -> p n f t", n=28)
            dst = gts[(LASTG, c)][:, row * 256:(row + 1) * 256].rearrange("p (f e t) -> p e f t", e=2, t=4)
            copy(out=dst[:, e], in_=src[:, n])

        def quant(g, c, r0, nr):
            key = (g % 2, c)
            a = (1 + r0) * ROW
            b = (1 + r0 + nr) * ROW
            nc.vector.quantize_mx(
                out=xq[key][:, a:b].bitcast(FP8X4),
                scales=xs[key][:, a:b],
                in_=gts[(g, c)][:, r0 * ROW * 4:(r0 + nr) * ROW * 4],
            )

        def quant_all(g, c):
            for r0, nr in (HALF_Q if g == LASTG else FULL_Q if g == 0 else WIDE_Q):
                quant(g, c, r0, nr)

        banks = {}

        def nbanks(g):
            return 6 if g == LASTG else 8

        def where(g, j):
            if g == 0:
                return j % 2, j // 2, FIRST_BANKS[j // 2]
            if g == LASTG:
                return j // 3, j % 3, HALF_BANKS[j % 3]
            return j // 4, j % 4, FULL_BANKS[j % 4]

        def passes(g, j, c):
            h, nb, (n0, nr) = where(g, j)
            if c == 0:
                banks[(g, j)] = psum.tile([P, 512], F32, name="ps", tag="ps")
            ps = banks[(g, j)]
            key = (g % 2, c)
            width = nr * ROW
            shift = 1 if g == LASTG else 0
            for k in range(K):
                col = k * 256 + h * 128
                a = (n0 + k + shift) * ROW
                nc.tensor.matmul_mx(
                    out=ps[:, 0:width],
                    lhsT=wq[:, c, col:col + 128].bitcast(FP8X4),
                    lhsT_scale=ws[:, c, col:col + 128],
                    rhs=xq[key][:, a:a + width].bitcast(FP8X4),
                    rhs_scale=xs[key][:, a:a + width],
                    start=(c == 0 and k == 0),
                    stop=(c == 1 and k == K - 1),
                )

        def combine(h, t4, later, before, result):
            nc.scalar.activation(out=later, in_=t4, func=ACT.Copy, scale=w1f[:, h, 1:2])
            nc.vector.scalar_tensor_tensor(out=result, in0=t4, scalar=w1f[:, h, 0:1], in1=before,
                                           op0=ALU.mult, op1=ALU.add)

        def halves(ap, u0, n0, nr):
            return ap.rearrange("p s n -> p (s n)").rearrange("p (u r) -> p u r", r=SPLIT)[:, u0:u0 + ROW, n0:n0 + nr]

        def epilogue(g, j):
            h, nb, (n0, nr) = where(g, j)
            f0 = GROUPS[g][0]
            ps = banks[(g, j)]
            if g == LASTG:
                combine(h, ps[:, 0:nr * ROW].rearrange("p (r u) -> p u r", u=ROW),
                        halves(ab[:, h], 2, n0, nr), halves(ab[:, h], 0, n0, nr),
                        halves(ot[:, h], 2 * f0 + 2, n0, nr))
            else:
                combine(h, ps[:, 0:nr * ROW].rearrange("p (n f) -> p f n", f=ROW),
                        ab[:, h, 1:ROW + 1, n0:n0 + nr], ab[:, h, 0:ROW, n0:n0 + nr],
                        ot[:, h, f0 + 1:f0 + ROW + 1, n0:n0 + nr])

        def store(h, m, r0, r1):
            nc.sync.dma_start(
                out=out[m, h * P:(h + 1) * P, r0:r1, :].rearrange("p l n -> p (l n)"),
                in_=ot[:, h, 28 * m + r0:28 * m + r1, :].rearrange("p s n -> p (s n)"),
            )

        EARLY = 24

        def store_pair(h, m0, m1):
            nc.sync.dma_start(
                out=out[m0:m1 + 1, h * P:(h + 1) * P, 0:2, :].rearrange("m p l n -> p m (l n)"),
                in_=ot[:, h, 28 * m0 + 28:28 * m1 + 56, :].rearrange(
                    "p (m s) n -> p m s n", s=28)[:, :, 0:2, :].rearrange("p m s n -> p m (s n)"),
            )

        def finish(g, hs):
            f0, ns = GROUPS[g]
            first = [m for m in range(M) if f0 <= 28 * m < f0 + ns]
            last = [m for m in range(M) if f0 <= 28 * m + 27 < f0 + ns]
            for h in range(hs.start, hs.stop):
                if g < LASTG:
                    nc.sync.dma_start(
                        out=out[last[0]:last[-1] + 1, h * P:(h + 1) * P, 2:28, :].rearrange("m p l n -> p m (l n)"),
                        in_=ot[:, h, 28 * last[0]:28 * last[-1] + 28, :].rearrange(
                            "p (m s) n -> p m s n", s=28)[:, :, 2:28, :].rearrange("p m s n -> p m (s n)"),
                    )
                else:
                    store(h, last[1], 2, 28)
                    store(h, last[0], EARLY, 28)
                if g == LASTG - 1:
                    store(h, last[-1] + 1, 2, EARLY)
            o = slice(28 * first[0] + 1, 28 * first[-1] + 2, 28)
            a = slice(28 * first[0] - f0, 28 * first[-1] - f0 + 1, 28)
            nc.vector.tensor_tensor(out=xx[:, hs, first[0]:first[-1] + 1, :], in0=ot[:, hs, o, :],
                                    in1=ab[:, hs, a, :], op=ALU.subtract)
            o = slice(28 * last[0] + 29, 28 * last[-1] + 30, 28)
            a = slice(28 * last[0] + 28 - f0, 28 * last[-1] + 29 - f0, 28)
            nc.vector.tensor_tensor(out=ot[:, hs, o, :], in0=xx[:, hs, last[0]:last[-1] + 1, :],
                                    in1=ab[:, hs, a, :], op=ALU.add)
            for h in range(hs.start, hs.stop):
                store_pair(h, last[0], last[-1])
            if g < LASTG:
                nc.scalar.copy(out=ab[:, hs, 0, :], in_=ab[:, hs, ns, :])

        vcopy = nc.vector.tensor_copy
        scopy = nc.scalar.copy

        for c in range(2):
            gts[(0, c)] = gtp.tile([P, 28 * ROW * 4], BF16, name="gt", tag="gt", align_bytes=64)
        regroup_w2(vcopy, 0, 0, 64)
        quant_w2(0, 0, 256)
        for s in range(2):
            regroup(vcopy, 0, 0, s, 0, 2)
            regroup(scopy, 0, 0, s, 2, 4)
            regroup(vcopy, 0, 0, s, 4, 6)
            regroup(scopy, 0, 0, s, 6, 7)
        regroup_w2(scopy, 0, 64, 128)
        regroup_w2(vcopy, 0, 128, 192)
        quant_w2(0, 256, 768)
        regroup(vcopy, 0, 0, 2, 0, 2)
        regroup(scopy, 0, 0, 2, 2, 7)
        quant_all(0, 0)
        regroup_w2(vcopy, 1, 0, 96)
        regroup_w2(scopy, 1, 96, 192)
        quant_w2(1, 0, 512)
        quant_w2(1, 512, 768)
        for s in range(2):
            regroup(vcopy, 0, 1, s, 0, 2)
            regroup(vcopy, 0, 1, s, 2, 3)
            regroup(scopy, 0, 1, s, 3, 7)
        regroup(vcopy, 0, 1, 2, 0, 2)
        regroup(scopy, 0, 1, 2, 2, 7)
        quant_all(0, 1)

        for m, c in ((3, 0), (4, 0), (3, 1), (4, 1), (5, 0), (6, 0), (5, 1), (6, 1)):
            load_x(m, c)
        load_half(0)
        load_half(1)

        for g in range(NG):
            nxt = g + 1
            n = nbanks(g)
            hooks = []
            if nxt < LASTG:
                for c in range(2):
                    gts[(nxt, c)] = gtp.tile([P, 28 * ROW * 4], BF16, name="gt", tag="gt", align_bytes=64)
                regroup(vcopy, nxt, 0, 1, 0, 6)
                regroup(scopy, nxt, 0, 0, 0, 7)
                regroup(vcopy, nxt, 0, 1, 6, 7)
                regroup(scopy, nxt, 0, 2, 0, 7)
                hooks = [(0, 0, 0, 4), (n // 4, 0, 4, 7), (n // 2, 2, 0, 4), ((5 * n) // 8, 2, 6, 7)]
            if nxt == LASTG:
                for c in range(2):
                    gth = gtp.tile([P, (SPLIT + 2) * ROW * 4], BF16, name="gth", tag="gt", align_bytes=64)
                    gts[(nxt, c)] = gth
                    nc.vector.memset(gth[:, 0:256], 0.0)
                    nc.vector.memset(gth[:, (SPLIT + 1) * 256:(SPLIT + 2) * 256], 0.0)
                regroup_half(vcopy, 0, 0, 2)
                regroup_half(scopy, 0, 2, 4)
                regroup_half(scopy, 0, 4, 7)
                halo_half(vcopy, 0, 0, 1, SPLIT - 1)
                halo_half(vcopy, 0, SPLIT + 1, 0, SPLIT)
            if g == 0:
                for j in range(n):
                    passes(g, j, 0)
            if nxt < NG:
                quant_all(nxt, 0)
            if nxt < LASTG:
                regroup(vcopy, nxt, 1, 1, 0, 6)
                regroup(vcopy, nxt, 1, 1, 6, 7)
                regroup(vcopy, nxt, 1, 2, 4, 6)
            if nxt == LASTG:
                regroup_half(vcopy, 1, 0, 2)
                regroup_half(scopy, 1, 2, 4)
                regroup_half(scopy, 1, 4, 7)
                halo_half(vcopy, 1, 0, 1, SPLIT - 1)
                halo_half(vcopy, 1, SPLIT + 1, 0, SPLIT)
            for j in range(n):
                if g > 0:
                    passes(g, j, 0)
                passes(g, j, 1)
                epilogue(g, j)
                for when, s, b0, b1 in hooks:
                    if when == j:
                        regroup(scopy, nxt, 1, s, b0, b1)
                if g == LASTG and j == n // 2 - 1:
                    finish(g, slice(0, 1))
                if nxt < NG and j == (3 * n) // 4:
                    quant_all(nxt, 1)
            finish(g, slice(1, 2) if g == LASTG else slice(0, 2))
